import numpy as np
import ml_dtypes


def mxq(x, axis, fmt="e4m3"):
    dtype, down = {"e4m3": (ml_dtypes.float8_e4m3fn, 7), "e5m2": (ml_dtypes.float8_e5m2, 14)}[fmt]
    v = np.moveaxis(np.asarray(x, np.float32).astype(ml_dtypes.bfloat16).astype(np.float64), axis, -1)
    blocks = v.reshape(v.shape[:-1] + (-1, 32))
    amax = np.abs(blocks).max(-1, keepdims=True)
    byte = np.maximum(np.where(amax > 0, np.frexp(amax)[1] - 1 + 127, 0) - down, 1)
    scale = np.exp2(byte - 127.0)
    codes = (blocks / scale).astype(np.float32).astype(dtype).astype(np.float64)
    return np.moveaxis((codes * scale).reshape(v.shape), -1, axis)


WIDE = False


def mx_kscale(k):
    if not WIDE:
        return np.ones(k)
    levels = np.array([10, -10, 5, -5, 0])
    if k % 512:
        return np.exp2(np.random.permutation(np.resize(levels, k // 32))).repeat(32)
    a = np.empty((k // 512, 16))
    for p in range(k // 512):
        a[p, :8] = np.random.permutation(np.resize(levels, 8))
        for g in range(8):
            far = levels[np.abs(levels - a[p, g]) >= 10]
            a[p, g + 8] = far[np.random.randint(len(far))]
    return np.exp2(a.ravel()).repeat(32)


BF16 = ml_dtypes.bfloat16


def bf(x):
    return np.asarray(x, np.float32).astype(BF16)


def f64(x):
    return np.asarray(x).astype(np.float64)


B, S, DIM, H, C, NOPE, ROPE, VDIM = 2, 512, 2048, 8, 512, 64, 128, 128
THETA = 10000.0
EPS = 1e-6


def rope_tables():
    freqs = 1.0 / THETA ** (np.arange(0, ROPE, 2, dtype=np.float64) / ROPE)
    ang = np.outer(np.arange(S, dtype=np.float64), freqs)
    return np.cos(ang), np.sin(ang)


def setup_inputs():
    s = mx_kscale(DIM)
    return {"x": bf(np.random.standard_normal((B, S, DIM)) * s),
            "wkv_a": bf(np.random.standard_normal((C + ROPE, DIM)) / np.sqrt(DIM) / s),
            "kv_norm_w": bf(1.0 + 0.1 * np.random.standard_normal(C))}


def reference(x, wkv_a, kv_norm_w):
    kv = mxq(f64(x), 2, "e4m3") @ mxq(f64(wkv_a), 1, "e4m3").T
    kv_lat, k_raw = kv[..., :C], kv[..., C:]
    cos, sin = rope_tables()
    x0, x1 = k_raw[..., 0::2], k_raw[..., 1::2]
    r0 = x0 * cos - x1 * sin
    r1 = x0 * sin + x1 * cos
    k_pe = np.stack([r0, r1], axis=-1).reshape(B, S, ROPE)
    rms = np.sqrt(np.mean(kv_lat * kv_lat, axis=-1, keepdims=True) + EPS)
    kv_cache = kv_lat / rms * f64(kv_norm_w)
    return kv_cache, k_pe

@@ -1,0 +1,321 @@
+import math
+
+import concourse.mybir as mybir
+from concourse.masks import make_identity
+
+F32 = mybir.dt.float32
+BF16 = mybir.dt.bfloat16
+I32 = mybir.dt.int32
+U32 = mybir.dt.uint32
+U8 = mybir.dt.uint8
+FP8X4 = mybir.dt.float8_e4m3fn_x4
+ALU = mybir.AluOpType
+ACT = mybir.ActivationFunctionType
+
+P = 128
+BATCH = 2
+SEQ = 512
+DIM = 2048
+LATENT = 512
+ROPE = 128
+PAIRS = ROPE // 2
+DOUBLINGS = 6
+assert 2**DOUBLINGS == PAIRS
+THETA = 10000.0
+EPS = 1e-6
+
+K_PASS = 4 * P
+PASSES = DIM // K_PASS
+WORDS = DIM // 2
+BLOCKS_PER_BANK = 4
+BANKS_PER_TILE = WORDS // P // BLOCKS_PER_BANK
+X_TILES = BATCH * SEQ // P
+SEQ_TILES = SEQ // P
+W_TILES = (LATENT + ROPE) // P
+
+FIRST_TOKEN_TILES = 2
+WARM_UP = 7
+
+TWO_PI = 2.0 * math.pi
+ROUND_MAGIC = 1.5 * 2.0**23
+
+FLOPS = 2 * BATCH * SEQ * DIM * (LATENT + ROPE)
+
+
+def tile_simplemla_pa_kernel(tc, x, wkv_a, kv_norm_w, out_0, out_1):
+    nc = tc.nc
+    x_rows = x.flatten_outer_dims()
+    kv_cache_rows = out_0.flatten_outer_dims()
+    k_pe_rows = out_1.flatten_outer_dims()
+
+    with (
+        tc.tile_pool(name="const", bufs=1) as const,
+        tc.tile_pool(name="raw", bufs=1) as raw,
+        tc.tile_pool(name="stage", bufs=3) as stage,
+        tc.tile_pool(name="quant", bufs=1) as quant,
+        tc.tile_pool(name="work", bufs=3) as work,
+        tc.psum_pool(name="psum_t", bufs=3) as psum_t,
+        tc.psum_pool(name="psum_lat", bufs=3) as psum_lat,
+        tc.psum_pool(name="psum_rope", bufs=2) as psum_rope,
+        tc.manual_schedule(),
+    ):
+        gain_rows = const.tile([P, LATENT], BF16)
+        nc.vector.memset(gain_rows[:], 0.0)
+        nc.scalar.dma_start(out=gain_rows[0:1, :], in_=kv_norm_w.rearrange("(o c) -> o c", o=1))
+
+        def load_rows(rows, name):
+            tile_of_rows = raw.tile([P, DIM], BF16, name=name)
+            nc.sync.dma_start(out=tile_of_rows[:], in_=rows)
+            return tile_of_rows
+
+        x_raw = {}
+        for m in range(FIRST_TOKEN_TILES):
+            x_raw[m] = load_rows(x_rows[m * P : (m + 1) * P, :], "x_raw%d" % m)
+        w_raw = {}
+        for n in range(W_TILES):
+            w_raw[n] = load_rows(wkv_a[n * P : (n + 1) * P, :], "w_raw%d" % n)
+        for m in range(FIRST_TOKEN_TILES, X_TILES):
+            x_raw[m] = load_rows(x_rows[m * P : (m + 1) * P, :], "x_raw%d" % m)
+
+        position_int = const.tile([P, SEQ_TILES], I32)
+        nc.gpsimd.iota(position_int[:], pattern=[[P, SEQ_TILES]], base=0, channel_multiplier=1)
+        identity = const.tile([P, P], F32)
+        make_identity(nc, identity[:])
+        ones = const.tile([P, P], BF16)
+        nc.vector.memset(ones[:], 1.0)
+        eps = const.tile([P, 1], F32)
+        nc.vector.memset(eps[:], EPS)
+
+        zeros = const.tile([P, LATENT], BF16)
+        nc.vector.memset(zeros[:], 0.0)
+        idle_bank = psum_lat.tile([P, LATENT], F32, name="latent")
+
+        def keep_clock_up():
+            nc.tensor.matmul(out=idle_bank[:], lhsT=ones[:], rhs=zeros[:], start=True, stop=True)
+
+        for warm in range(WARM_UP):
+            keep_clock_up()
+
+        position = const.tile([P, SEQ_TILES], F32)
+        nc.vector.tensor_copy(out=position[:], in_=position_int[:])
+        frequency = const.tile([P, PAIRS], F32)
+        nc.vector.memset(frequency[:, 0:1], 1.0)
+        for doubling in range(DOUBLINGS):
+            n = 2**doubling
+            nc.vector.tensor_scalar(
+                out=frequency[:, n : 2 * n],
+                in0=frequency[:, 0:n],
+                scalar1=THETA ** (-n / PAIRS),
+                scalar2=None,
+                op0=ALU.mult,
+            )
+        table_shape = [P, SEQ_TILES, PAIRS]
+        turns = const.tile([P, 2, SEQ_TILES, PAIRS], F32)
+        nc.vector.scalar_tensor_tensor(
+            out=turns[:, 0],
+            in0=frequency[:].unsqueeze(1).to_broadcast(table_shape),
+            scalar=1.0 / TWO_PI,
+            in1=position[:].unsqueeze(2).to_broadcast(table_shape),
+            op0=ALU.mult,
+            op1=ALU.mult,
+        )
+        nc.vector.tensor_scalar(
+            out=turns[:, 1], in0=turns[:, 0], scalar1=0.25, scalar2=None, op0=ALU.add
+        )
+        whole_turns = const.tile([P, 2, SEQ_TILES, PAIRS], F32)
+        nc.vector.tensor_scalar(
+            out=whole_turns[:],
+            in0=turns[:],
+            scalar1=ROUND_MAGIC,
+            scalar2=ROUND_MAGIC,
+            op0=ALU.add,
+            op1=ALU.subtract,
+        )
+        part_turns = const.tile([P, 2, SEQ_TILES * PAIRS], F32)
+        nc.vector.tensor_tensor(
+            out=part_turns[:].rearrange("p s c -> p (s c)"),
+            in0=turns[:].rearrange("p s t j -> p (s t j)"),
+            in1=whole_turns[:].rearrange("p s t j -> p (s t j)"),
+            op=ALU.subtract,
+        )
+        sin_table = const.tile([P, SEQ_TILES, PAIRS], F32)
+        nc.scalar.activation(
+            out=sin_table[:].rearrange("p t j -> p (t j)"),
+            in_=part_turns[:, 0, :],
+            func=ACT.Sin,
+            scale=TWO_PI,
+        )
+        cos_pairs = const.tile([P, SEQ_TILES, PAIRS, 2], F32)
+        nc.scalar.activation(
+            out=cos_pairs[:].rearrange("p t j e -> p (t j) e"),
+            in_=part_turns[:, 1, :].unsqueeze(2).to_broadcast([P, SEQ_TILES * PAIRS, 2]),
+            func=ACT.Sin,
+            scale=TWO_PI,
+        )
+        table_warmer = const.tile([P, 1], F32)
+        nc.scalar.activation(out=table_warmer[:], in_=eps[:], func=ACT.Abs_reciprocal_sqrt)
+
+        def transpose_rows(rows, copies):
+            words = rows[:].bitcast(F32)
+            grouped = stage.tile([P, PASSES * P * 4], BF16, align_bytes=64)
+            grouped_words = grouped[:].bitcast(F32).rearrange(
+                "p (g r u) -> p g r u", g=PASSES, u=2
+            )
+            for h in range(BANKS_PER_TILE):
+                bank = psum_t.tile([P, 2, 2, P], F32, tag="bank")
+                for g in range(2):
+                    for u in range(2):
+                        first = (2 * h + g) * 2 * P
+                        nc.tensor.transpose(
+                            bank[:, g, u, :],
+                            words[:, first + u : first + 2 * P : 2],
+                            identity[:],
+                        )
+                copies[h](
+                    out=grouped_words[:, 2 * h : 2 * h + 2],
+                    in_=bank[:].rearrange("p g u r -> p g r u"),
+                )
+            return grouped
+
+        w_codes = quant.tile([P, PASSES, LATENT + ROPE], U32, align_bytes=64)
+        w_scales = quant.tile([P, PASSES, LATENT + ROPE], U8, align_bytes=64)
+
+        def quantise_weights(n, grouped):
+            for g in range(PASSES):
+                nc.vector.quantize_mx(
+                    out=w_codes[:, g, n * P : (n + 1) * P].bitcast(FP8X4),
+                    scales=w_scales[:, g, n * P : (n + 1) * P],
+                    in_=grouped[:, g * 4 * P : (g + 1) * 4 * P],
+                )
+
+        x_codes = {}
+        x_scales = {}
+
+        def quantise_tokens(m, grouped):
+            x_codes[m] = quant.tile([P, PASSES * P], U32, align_bytes=64, name="x_codes", bufs=3)
+            x_scales[m] = quant.tile([P, PASSES * P], U8, align_bytes=64, name="x_scales", bufs=3)
+            nc.vector.quantize_mx(
+                out=x_codes[m][:].bitcast(FP8X4), scales=x_scales[m][:], in_=grouped[:]
+            )
+
+        def multiply(m, out, columns):
+            for g in range(PASSES):
+                nc.tensor.matmul_mx(
+                    out=out,
+                    lhsT=x_codes[m][:, g * P : (g + 1) * P].bitcast(FP8X4),
+                    lhsT_scale=x_scales[m][:, g * P : (g + 1) * P],
+                    rhs=w_codes[:, g, columns].bitcast(FP8X4),
+                    rhs_scale=w_scales[:, g, columns],
+                    start=(g == 0),
+                    stop=(g == PASSES - 1),
+                )
+
+        def inverse_root_mean_square(latent):
+            squares = work.tile([P, LATENT], BF16)
+            sum_squares = work.tile([P, 1], F32)
+            nc.scalar.activation(
+                out=squares[:], in_=latent[:], func=ACT.Square, accum_out=sum_squares[:]
+            )
+            inverse_rms = work.tile([P, 1], F32)
+            nc.scalar.activation(
+                out=inverse_rms[:],
+                in_=sum_squares[:],
+                func=ACT.Abs_reciprocal_sqrt,
+                scale=1.0 / LATENT,
+                bias=eps[:, 0:1],
+            )
+            return inverse_rms
+
+        def normalise(m, latent, inverse_rms):
+            kv_cache = work.tile([P, LATENT], F32, bufs=4)
+            nc.vector.scalar_tensor_tensor(
+                out=kv_cache[:],
+                in0=latent[:],
+                scalar=inverse_rms[:, 0:1],
+                in1=gain[:],
+                op0=ALU.mult,
+                op1=ALU.mult,
+            )
+            nc.sync.dma_start(out=kv_cache_rows[m * P : (m + 1) * P, :], in_=kv_cache[:])
+
+        def rotation_products(t, raw_keys):
+            pairs = raw_keys[:].rearrange("p t (j e) -> p (t j) e", e=2)
+            sines = sin_table[:, t : t + 2].rearrange("p t j -> p (t j)")
+            with_cos = work.tile([P, 2 * PAIRS, 2], F32)
+            nc.vector.tensor_tensor(
+                out=with_cos[:],
+                in0=pairs,
+                in1=cos_pairs[:, t : t + 2].rearrange("p t j e -> p (t j) e"),
+                op=ALU.mult,
+            )
+            with_sin = work.tile([P, 2, 2 * PAIRS], F32)
+            nc.vector.scalar_tensor_tensor(
+                out=with_sin[:, 0, :],
+                in0=pairs[:, :, 1],
+                scalar=-1.0,
+                in1=sines,
+                op0=ALU.mult,
+                op1=ALU.mult,
+            )
+            nc.vector.tensor_tensor(
+                out=with_sin[:, 1, :], in0=pairs[:, :, 0], in1=sines, op=ALU.mult
+            )
+            return with_cos, with_sin
+
+        def rotation_sum(m, with_cos, with_sin):
+            k_pe = work.tile([P, 2 * PAIRS, 2], F32)
+            nc.vector.tensor_tensor(
+                out=k_pe[:], in0=with_cos[:], in1=with_sin[:].rearrange("p e c -> p c e"), op=ALU.add
+            )
+            nc.sync.dma_start(
+                out=k_pe_rows[m * P : (m + 2) * P, :].rearrange("(t p) c -> p t c", p=P),
+                in_=k_pe[:].rearrange("p (t j) e -> p t (j e)", t=2),
+            )
+
+        shared_copies = [nc.vector.tensor_copy, nc.scalar.copy]
+        scalar_copies = [nc.scalar.copy, nc.scalar.copy]
+
+        def transpose_early(rows):
+            grouped = transpose_rows(rows, shared_copies)
+            keep_clock_up()
+            return grouped
+
+        grouped_x = {}
+        grouped_x[0] = transpose_early(x_raw[0])
+        grouped_x[1] = transpose_early(x_raw[1])
+        quantise_tokens(0, grouped_x[0])
+        grouped_w = {}
+        grouped_w[0] = transpose_early(w_raw[0])
+        quantise_tokens(1, grouped_x[1])
+        for n in range(1, W_TILES):
+            grouped_w[n] = transpose_early(w_raw[n])
+            quantise_weights(n - 1, grouped_w[n - 1])
+        quantise_weights(W_TILES - 1, grouped_w[W_TILES - 1])
+
+        gain_bank = psum_t.tile([P, LATENT], F32, tag="bank")
+        nc.tensor.matmul(out=gain_bank[:], lhsT=ones[:], rhs=gain_rows[:], start=True, stop=True)
+        gain = const.tile([P, LATENT], F32)
+        nc.vector.tensor_copy(out=gain[:], in_=gain_bank[:])
+
+        latent = {}
+        inverse_rms = {}
+        raw_keys = None
+        for m in range(X_TILES + 1):
+            if m < X_TILES:
+                latent[m] = psum_lat.tile([P, LATENT], F32, name="latent")
+                multiply(m, latent[m][:], slice(0, LATENT))
+                if m % 2 == 0:
+                    raw_keys = psum_rope.tile([P, 2, ROPE], F32)
+                multiply(m, raw_keys[:, m % 2, :], slice(LATENT, LATENT + ROPE))
+            if m > 0:
+                inverse_rms[m - 1] = inverse_root_mean_square(latent[m - 1])
+            if m + 2 < X_TILES:
+                grouped_x[m + 2] = transpose_rows(x_raw[m + 2], scalar_copies)
+            if FIRST_TOKEN_TILES <= m + 1 < X_TILES:
+                quantise_tokens(m + 1, grouped_x[m + 1])
+            if m > 0:
+                normalise(m - 1, latent[m - 1], inverse_rms[m - 1])
+            if m % 2 == 1:
+                with_cos, with_sin = rotation_products((m - 1) % SEQ_TILES, raw_keys)
+            if m % 2 == 0 and m > 0:
+                rotation_sum(m - 2, with_cos, with_sin)

@@ -33,7 +33,7 @@ X_TILES = BATCH * SEQ // P
 SEQ_TILES = SEQ // P
 W_TILES = (LATENT + ROPE) // P
 
-FIRST_TOKEN_TILES = 2
+AHEAD = 3
 WARM_UP = 7
 
 TWO_PI = 2.0 * math.pi
@@ -51,7 +51,7 @@ def tile_simplemla_pa_kernel(tc, x, wkv_a, kv_norm_w, out_0, out_1):
     with (
         tc.tile_pool(name="const", bufs=1) as const,
         tc.tile_pool(name="raw", bufs=1) as raw,
-        tc.tile_pool(name="stage", bufs=3) as stage,
+        tc.tile_pool(name="stage", bufs=4) as stage,
         tc.tile_pool(name="quant", bufs=1) as quant,
         tc.tile_pool(name="work", bufs=3) as work,
         tc.psum_pool(name="psum_t", bufs=3) as psum_t,
@@ -68,13 +68,11 @@ def tile_simplemla_pa_kernel(tc, x, wkv_a, kv_norm_w, out_0, out_1):
             nc.sync.dma_start(out=tile_of_rows[:], in_=rows)
             return tile_of_rows
 
-        x_raw = {}
-        for m in range(FIRST_TOKEN_TILES):
-            x_raw[m] = load_rows(x_rows[m * P : (m + 1) * P, :], "x_raw%d" % m)
         w_raw = {}
         for n in range(W_TILES):
             w_raw[n] = load_rows(wkv_a[n * P : (n + 1) * P, :], "w_raw%d" % n)
-        for m in range(FIRST_TOKEN_TILES, X_TILES):
+        x_raw = {}
+        for m in range(X_TILES):
             x_raw[m] = load_rows(x_rows[m * P : (m + 1) * P, :], "x_raw%d" % m)
 
         position_int = const.tile([P, SEQ_TILES], I32)
@@ -192,8 +190,8 @@ def tile_simplemla_pa_kernel(tc, x, wkv_a, kv_norm_w, out_0, out_1):
         x_scales = {}
 
         def quantise_tokens(m, grouped):
-            x_codes[m] = quant.tile([P, PASSES * P], U32, align_bytes=64, name="x_codes", bufs=3)
-            x_scales[m] = quant.tile([P, PASSES * P], U8, align_bytes=64, name="x_scales", bufs=3)
+            x_codes[m] = quant.tile([P, PASSES * P], U32, align_bytes=64, name="x_codes", bufs=AHEAD + 1)
+            x_scales[m] = quant.tile([P, PASSES * P], U8, align_bytes=64, name="x_scales", bufs=AHEAD + 1)
             nc.vector.quantize_mx(
                 out=x_codes[m][:].bitcast(FP8X4), scales=x_scales[m][:], in_=grouped[:]
             )
@@ -280,17 +278,18 @@ def tile_simplemla_pa_kernel(tc, x, wkv_a, kv_norm_w, out_0, out_1):
             keep_clock_up()
             return grouped
 
-        grouped_x = {}
-        grouped_x[0] = transpose_early(x_raw[0])
-        grouped_x[1] = transpose_early(x_raw[1])
-        quantise_tokens(0, grouped_x[0])
         grouped_w = {}
-        grouped_w[0] = transpose_early(w_raw[0])
-        quantise_tokens(1, grouped_x[1])
-        for n in range(1, W_TILES):
+        for n in range(W_TILES):
             grouped_w[n] = transpose_early(w_raw[n])
-            quantise_weights(n - 1, grouped_w[n - 1])
-        quantise_weights(W_TILES - 1, grouped_w[W_TILES - 1])
+            if n > 0:
+                quantise_weights(n - 1, grouped_w[n - 1])
+        grouped_x = {}
+        for m in range(AHEAD):
+            grouped_x[m] = transpose_rows(x_raw[m], shared_copies)
+            if m == 0:
+                quantise_weights(W_TILES - 1, grouped_w[W_TILES - 1])
+            else:
+                quantise_tokens(m - 1, grouped_x[m - 1])
 
         gain_bank = psum_t.tile([P, LATENT], F32, tag="bank")
         nc.tensor.matmul(out=gain_bank[:], lhsT=ones[:], rhs=gain_rows[:], start=True, stop=True)
@@ -309,10 +308,10 @@ def tile_simplemla_pa_kernel(tc, x, wkv_a, kv_norm_w, out_0, out_1):
                 multiply(m, raw_keys[:, m % 2, :], slice(LATENT, LATENT + ROPE))
             if m > 0:
                 inverse_rms[m - 1] = inverse_root_mean_square(latent[m - 1])
-            if m + 2 < X_TILES:
-                grouped_x[m + 2] = transpose_rows(x_raw[m + 2], scalar_copies)
-            if FIRST_TOKEN_TILES <= m + 1 < X_TILES:
-                quantise_tokens(m + 1, grouped_x[m + 1])
+            if m + AHEAD < X_TILES:
+                grouped_x[m + AHEAD] = transpose_rows(x_raw[m + AHEAD], scalar_copies)
+            if m + AHEAD - 1 < X_TILES:
+                quantise_tokens(m + AHEAD - 1, grouped_x[m + AHEAD - 1])
             if m > 0:
                 normalise(m - 1, latent[m - 1], inverse_rms[m - 1])
             if m % 2 == 1:

@@ -19,8 +19,9 @@ DIM = 2048
 LATENT = 512
 ROPE = 128
 PAIRS = ROPE // 2
-DOUBLINGS = 6
-assert 2**DOUBLINGS == PAIRS
+DOUBLINGS = 3
+STEPS = 2**DOUBLINGS
+assert STEPS * STEPS == PAIRS
 THETA = 10000.0
 EPS = 1e-6
 
@@ -34,7 +35,7 @@ SEQ_TILES = SEQ // P
 W_TILES = (LATENT + ROPE) // P
 
 AHEAD = 3
-WARM_UP = 7
+WARM_UP = 3
 
 TWO_PI = 2.0 * math.pi
 ROUND_MAGIC = 1.5 * 2.0**23
@@ -59,9 +60,6 @@ def tile_simplemla_pa_kernel(tc, x, wkv_a, kv_norm_w, out_0, out_1):
         tc.psum_pool(name="psum_rope", bufs=2) as psum_rope,
         tc.manual_schedule(),
     ):
-        gain_rows = const.tile([P, LATENT], BF16)
-        nc.vector.memset(gain_rows[:], 0.0)
-        nc.scalar.dma_start(out=gain_rows[0:1, :], in_=kv_norm_w.rearrange("(o c) -> o c", o=1))
 
         def load_rows(rows, name):
             tile_of_rows = raw.tile([P, DIM], BF16, name=name)
@@ -75,17 +73,25 @@ def tile_simplemla_pa_kernel(tc, x, wkv_a, kv_norm_w, out_0, out_1):
         for m in range(X_TILES):
             x_raw[m] = load_rows(x_rows[m * P : (m + 1) * P, :], "x_raw%d" % m)
 
-        position_int = const.tile([P, SEQ_TILES], I32)
-        nc.gpsimd.iota(position_int[:], pattern=[[P, SEQ_TILES]], base=0, channel_multiplier=1)
+        position = const.tile([P, SEQ_TILES], F32)
+        nc.gpsimd.iota(
+            position[:],
+            pattern=[[P, SEQ_TILES]],
+            base=0,
+            channel_multiplier=1,
+            allow_small_or_imprecise_dtypes=True,
+        )
         identity = const.tile([P, P], F32)
         make_identity(nc, identity[:])
+        gain_rows = const.tile([P, LATENT], BF16)
+        nc.gpsimd.memset(gain_rows[:], 0.0)
         ones = const.tile([P, P], BF16)
         nc.vector.memset(ones[:], 1.0)
+        zeros = const.tile([P, LATENT], BF16)
+        nc.vector.memset(zeros[:], 0.0)
         eps = const.tile([P, 1], F32)
         nc.vector.memset(eps[:], EPS)
 
-        zeros = const.tile([P, LATENT], BF16)
-        nc.vector.memset(zeros[:], 0.0)
         idle_bank = psum_lat.tile([P, LATENT], F32, name="latent")
 
         def keep_clock_up():
@@ -94,33 +100,44 @@ def tile_simplemla_pa_kernel(tc, x, wkv_a, kv_norm_w, out_0, out_1):
         for warm in range(WARM_UP):
             keep_clock_up()
 
-        position = const.tile([P, SEQ_TILES], F32)
-        nc.vector.tensor_copy(out=position[:], in_=position_int[:])
-        frequency = const.tile([P, PAIRS], F32)
-        nc.vector.memset(frequency[:, 0:1], 1.0)
+        table_warmer = const.tile([P, 1], F32)
+        nc.scalar.activation(out=table_warmer[:], in_=eps[:], func=ACT.Sin)
+        powers = const.tile([P, 2, STEPS], F32)
+        nc.vector.memset(powers[:, :, 0:1], 1.0)
         for doubling in range(DOUBLINGS):
             n = 2**doubling
-            nc.vector.tensor_scalar(
-                out=frequency[:, n : 2 * n],
-                in0=frequency[:, 0:n],
-                scalar1=THETA ** (-n / PAIRS),
-                scalar2=None,
-                op0=ALU.mult,
-            )
-        table_shape = [P, SEQ_TILES, PAIRS]
-        turns = const.tile([P, 2, SEQ_TILES, PAIRS], F32)
+            for plane, step in ((0, STEPS), (1, 1)):
+                nc.vector.tensor_scalar(
+                    out=powers[:, plane, n : 2 * n],
+                    in0=powers[:, plane, 0:n],
+                    scalar1=THETA ** (-n * step / PAIRS),
+                    scalar2=None,
+                    op0=ALU.mult,
+                )
+        half_pi = const.tile([P, 1], F32)
+        nc.vector.tensor_scalar(
+            out=half_pi[:], in0=powers[:, 0, 0:1], scalar1=TWO_PI / 4, scalar2=None, op0=ALU.mult
+        )
+        coarse_turns = const.tile([P, SEQ_TILES, STEPS], F32)
         nc.vector.scalar_tensor_tensor(
-            out=turns[:, 0],
-            in0=frequency[:].unsqueeze(1).to_broadcast(table_shape),
+            out=coarse_turns[:],
+            in0=powers[:, 0, :].unsqueeze(1).to_broadcast([P, SEQ_TILES, STEPS]),
             scalar=1.0 / TWO_PI,
-            in1=position[:].unsqueeze(2).to_broadcast(table_shape),
+            in1=position[:].unsqueeze(2).to_broadcast([P, SEQ_TILES, STEPS]),
             op0=ALU.mult,
             op1=ALU.mult,
         )
-        nc.vector.tensor_scalar(
-            out=turns[:, 1], in0=turns[:, 0], scalar1=0.25, scalar2=None, op0=ALU.add
+        turns = const.tile([P, SEQ_TILES * PAIRS], F32)
+        nc.vector.tensor_tensor(
+            out=turns[:].rearrange("p (c b) -> p c b", b=STEPS),
+            in0=coarse_turns[:]
+            .rearrange("p t a -> p (t a)")
+            .unsqueeze(2)
+            .to_broadcast([P, SEQ_TILES * STEPS, STEPS]),
+            in1=powers[:, 1, :].unsqueeze(1).to_broadcast([P, SEQ_TILES * STEPS, STEPS]),
+            op=ALU.mult,
         )
-        whole_turns = const.tile([P, 2, SEQ_TILES, PAIRS], F32)
+        whole_turns = const.tile([P, SEQ_TILES * PAIRS], F32)
         nc.vector.tensor_scalar(
             out=whole_turns[:],
             in0=turns[:],
@@ -129,32 +146,45 @@ def tile_simplemla_pa_kernel(tc, x, wkv_a, kv_norm_w, out_0, out_1):
             op0=ALU.add,
             op1=ALU.subtract,
         )
-        part_turns = const.tile([P, 2, SEQ_TILES * PAIRS], F32)
+        part_turns = const.tile([P, SEQ_TILES * PAIRS], F32)
         nc.vector.tensor_tensor(
-            out=part_turns[:].rearrange("p s c -> p (s c)"),
-            in0=turns[:].rearrange("p s t j -> p (s t j)"),
-            in1=whole_turns[:].rearrange("p s t j -> p (s t j)"),
-            op=ALU.subtract,
+            out=part_turns[:], in0=turns[:], in1=whole_turns[:], op=ALU.subtract
+        )
+        minus_size = const.tile([P, SEQ_TILES * PAIRS], F32)
+        nc.vector.scalar_tensor_tensor(
+            out=minus_size[:],
+            in0=part_turns[:],
+            scalar=-1.0,
+            in1=part_turns[:],
+            op0=ALU.mult,
+            op1=ALU.min,
         )
         sin_table = const.tile([P, SEQ_TILES, PAIRS], F32)
         nc.scalar.activation(
             out=sin_table[:].rearrange("p t j -> p (t j)"),
-            in_=part_turns[:, 0, :],
+            in_=part_turns[:],
             func=ACT.Sin,
             scale=TWO_PI,
         )
         cos_pairs = const.tile([P, SEQ_TILES, PAIRS, 2], F32)
         nc.scalar.activation(
             out=cos_pairs[:].rearrange("p t j e -> p (t j) e"),
-            in_=part_turns[:, 1, :].unsqueeze(2).to_broadcast([P, SEQ_TILES * PAIRS, 2]),
+            in_=minus_size[:].unsqueeze(2).to_broadcast([P, SEQ_TILES * PAIRS, 2]),
             func=ACT.Sin,
             scale=TWO_PI,
+            bias=half_pi[:, 0:1],
         )
-        table_warmer = const.tile([P, 1], F32)
         nc.scalar.activation(out=table_warmer[:], in_=eps[:], func=ACT.Abs_reciprocal_sqrt)
+        nc.scalar.dma_start(out=gain_rows[0:1, :], in_=kv_norm_w.rearrange("(o c) -> o c", o=1))
 
-        def transpose_rows(rows, copies):
-            words = rows[:].bitcast(F32)
+        def sort_words(rows, name):
+            ordered = raw.tile([P, PASSES, 2, P], F32, name=name)
+            words = rows[:].bitcast(F32).rearrange("p (g q u) -> p g u q", g=PASSES, u=2)
+            for g in range(PASSES):
+                nc.gpsimd.tensor_copy(out=ordered[:, g], in_=words[:, g])
+            return ordered
+
+        def transpose_rows(blocks, copies):
             grouped = stage.tile([P, PASSES * P * 4], BF16, align_bytes=64)
             grouped_words = grouped[:].bitcast(F32).rearrange(
                 "p (g r u) -> p g r u", g=PASSES, u=2
@@ -163,17 +193,21 @@ def tile_simplemla_pa_kernel(tc, x, wkv_a, kv_norm_w, out_0, out_1):
                 bank = psum_t.tile([P, 2, 2, P], F32, tag="bank")
                 for g in range(2):
                     for u in range(2):
-                        first = (2 * h + g) * 2 * P
                         nc.tensor.transpose(
-                            bank[:, g, u, :],
-                            words[:, first + u : first + 2 * P : 2],
-                            identity[:],
+                            bank[:, g, u, :], blocks(2 * h + g, u), identity[:]
                         )
                 copies[h](
                     out=grouped_words[:, 2 * h : 2 * h + 2],
                     in_=bank[:].rearrange("p g u r -> p g r u"),
                 )
             return grouped
+
+        def as_loaded(rows):
+            words = rows[:].bitcast(F32).rearrange("p (g q u) -> p g u q", g=PASSES, u=2)
+            return lambda g, u: words[:, g, u, :]
+
+        def as_sorted(ordered):
+            return lambda g, u: ordered[:, g, u, :]
 
         w_codes = quant.tile([P, PASSES, LATENT + ROPE], U32, align_bytes=64)
         w_scales = quant.tile([P, PASSES, LATENT + ROPE], U8, align_bytes=64)
@@ -272,24 +306,29 @@ def tile_simplemla_pa_kernel(tc, x, wkv_a, kv_norm_w, out_0, out_1):
 
         shared_copies = [nc.vector.tensor_copy, nc.scalar.copy]
         scalar_copies = [nc.scalar.copy, nc.scalar.copy]
+        vector_copies = [nc.vector.tensor_copy, nc.vector.tensor_copy]
 
-        def transpose_early(rows):
-            grouped = transpose_rows(rows, shared_copies)
+        def transpose_early(rows, copies):
+            grouped = transpose_rows(as_loaded(rows), copies)
             keep_clock_up()
             return grouped
 
         grouped_w = {}
         for n in range(W_TILES):
-            grouped_w[n] = transpose_early(w_raw[n])
+            grouped_w[n] = transpose_early(w_raw[n], vector_copies if n == 0 else shared_copies)
             if n > 0:
                 quantise_weights(n - 1, grouped_w[n - 1])
         grouped_x = {}
         for m in range(AHEAD):
-            grouped_x[m] = transpose_rows(x_raw[m], shared_copies)
+            grouped_x[m] = transpose_rows(as_loaded(x_raw[m]), shared_copies)
             if m == 0:
                 quantise_weights(W_TILES - 1, grouped_w[W_TILES - 1])
             else:
                 quantise_tokens(m - 1, grouped_x[m - 1])
+
+        x_sorted = {}
+        for m in range(AHEAD, X_TILES):
+            x_sorted[m] = sort_words(x_raw[m], "x_sorted%d" % m)
 
         gain_bank = psum_t.tile([P, LATENT], F32, tag="bank")
         nc.tensor.matmul(out=gain_bank[:], lhsT=ones[:], rhs=gain_rows[:], start=True, stop=True)
@@ -309,7 +348,9 @@ def tile_simplemla_pa_kernel(tc, x, wkv_a, kv_norm_w, out_0, out_1):
             if m > 0:
                 inverse_rms[m - 1] = inverse_root_mean_square(latent[m - 1])
             if m + AHEAD < X_TILES:
-                grouped_x[m + AHEAD] = transpose_rows(x_raw[m + AHEAD], scalar_copies)
+                grouped_x[m + AHEAD] = transpose_rows(
+                    as_sorted(x_sorted[m + AHEAD]), scalar_copies
+                )
             if m + AHEAD - 1 < X_TILES:
                 quantise_tokens(m + AHEAD - 1, grouped_x[m + AHEAD - 1])
             if m > 0:

@@ -177,13 +177,6 @@ def tile_simplemla_pa_kernel(tc, x, wkv_a, kv_norm_w, out_0, out_1):
         nc.scalar.activation(out=table_warmer[:], in_=eps[:], func=ACT.Abs_reciprocal_sqrt)
         nc.scalar.dma_start(out=gain_rows[0:1, :], in_=kv_norm_w.rearrange("(o c) -> o c", o=1))
 
-        def sort_words(rows, name):
-            ordered = raw.tile([P, PASSES, 2, P], F32, name=name)
-            words = rows[:].bitcast(F32).rearrange("p (g q u) -> p g u q", g=PASSES, u=2)
-            for g in range(PASSES):
-                nc.gpsimd.tensor_copy(out=ordered[:, g], in_=words[:, g])
-            return ordered
-
         def transpose_rows(blocks, copies):
             grouped = stage.tile([P, PASSES * P * 4], BF16, align_bytes=64)
             grouped_words = grouped[:].bitcast(F32).rearrange(
@@ -205,9 +198,6 @@ def tile_simplemla_pa_kernel(tc, x, wkv_a, kv_norm_w, out_0, out_1):
         def as_loaded(rows):
             words = rows[:].bitcast(F32).rearrange("p (g q u) -> p g u q", g=PASSES, u=2)
             return lambda g, u: words[:, g, u, :]
-
-        def as_sorted(ordered):
-            return lambda g, u: ordered[:, g, u, :]
 
         w_codes = quant.tile([P, PASSES, LATENT + ROPE], U32, align_bytes=64)
         w_scales = quant.tile([P, PASSES, LATENT + ROPE], U8, align_bytes=64)
@@ -326,10 +316,6 @@ def tile_simplemla_pa_kernel(tc, x, wkv_a, kv_norm_w, out_0, out_1):
             else:
                 quantise_tokens(m - 1, grouped_x[m - 1])
 
-        x_sorted = {}
-        for m in range(AHEAD, X_TILES):
-            x_sorted[m] = sort_words(x_raw[m], "x_sorted%d" % m)
-
         gain_bank = psum_t.tile([P, LATENT], F32, tag="bank")
         nc.tensor.matmul(out=gain_bank[:], lhsT=ones[:], rhs=gain_rows[:], start=True, stop=True)
         gain = const.tile([P, LATENT], F32)
@@ -349,7 +335,7 @@ def tile_simplemla_pa_kernel(tc, x, wkv_a, kv_norm_w, out_0, out_1):
                 inverse_rms[m - 1] = inverse_root_mean_square(latent[m - 1])
             if m + AHEAD < X_TILES:
                 grouped_x[m + AHEAD] = transpose_rows(
-                    as_sorted(x_sorted[m + AHEAD]), scalar_copies
+                    as_loaded(x_raw[m + AHEAD]), scalar_copies
                 )
             if m + AHEAD - 1 < X_TILES:
                 quantise_tokens(m + AHEAD - 1, grouped_x[m + AHEAD - 1])

@@ -34,7 +34,8 @@ X_TILES = BATCH * SEQ // P
 SEQ_TILES = SEQ // P
 W_TILES = (LATENT + ROPE) // P
 
-AHEAD = 3
+FIRST_TILES = 2
+LEAD = 3
 WARM_UP = 3
 
 TWO_PI = 2.0 * math.pi
@@ -55,9 +56,9 @@ def tile_simplemla_pa_kernel(tc, x, wkv_a, kv_norm_w, out_0, out_1):
         tc.tile_pool(name="stage", bufs=4) as stage,
         tc.tile_pool(name="quant", bufs=1) as quant,
         tc.tile_pool(name="work", bufs=3) as work,
-        tc.psum_pool(name="psum_t", bufs=3) as psum_t,
+        tc.psum_pool(name="psum_t", bufs=4) as psum_t,
         tc.psum_pool(name="psum_lat", bufs=3) as psum_lat,
-        tc.psum_pool(name="psum_rope", bufs=2) as psum_rope,
+        tc.psum_pool(name="psum_rope", bufs=1) as psum_rope,
         tc.manual_schedule(),
     ):
 
@@ -66,11 +67,13 @@ def tile_simplemla_pa_kernel(tc, x, wkv_a, kv_norm_w, out_0, out_1):
             nc.sync.dma_start(out=tile_of_rows[:], in_=rows)
             return tile_of_rows
 
+        x_raw = {}
+        for m in range(FIRST_TILES):
+            x_raw[m] = load_rows(x_rows[m * P : (m + 1) * P, :], "x_raw%d" % m)
         w_raw = {}
         for n in range(W_TILES):
             w_raw[n] = load_rows(wkv_a[n * P : (n + 1) * P, :], "w_raw%d" % n)
-        x_raw = {}
-        for m in range(X_TILES):
+        for m in range(FIRST_TILES, X_TILES):
             x_raw[m] = load_rows(x_rows[m * P : (m + 1) * P, :], "x_raw%d" % m)
 
         position = const.tile([P, SEQ_TILES], F32)
@@ -214,8 +217,8 @@ def tile_simplemla_pa_kernel(tc, x, wkv_a, kv_norm_w, out_0, out_1):
         x_scales = {}
 
         def quantise_tokens(m, grouped):
-            x_codes[m] = quant.tile([P, PASSES * P], U32, align_bytes=64, name="x_codes", bufs=AHEAD + 1)
-            x_scales[m] = quant.tile([P, PASSES * P], U8, align_bytes=64, name="x_scales", bufs=AHEAD + 1)
+            x_codes[m] = quant.tile([P, PASSES * P], U32, align_bytes=64, name="x_codes", bufs=X_TILES)
+            x_scales[m] = quant.tile([P, PASSES * P], U8, align_bytes=64, name="x_scales", bufs=X_TILES)
             nc.vector.quantize_mx(
                 out=x_codes[m][:].bitcast(FP8X4), scales=x_scales[m][:], in_=grouped[:]
             )
@@ -294,54 +297,72 @@ def tile_simplemla_pa_kernel(tc, x, wkv_a, kv_norm_w, out_0, out_1):
                 in_=k_pe[:].rearrange("p (t j) e -> p t (j e)", t=2),
             )
 
+        order = [("x", m) for m in range(FIRST_TILES)]
+        order += [("w", n) for n in range(W_TILES)]
+        order += [("x", m) for m in range(FIRST_TILES, X_TILES)]
+        vector_copies = [nc.vector.tensor_copy, nc.vector.tensor_copy]
         shared_copies = [nc.vector.tensor_copy, nc.scalar.copy]
         scalar_copies = [nc.scalar.copy, nc.scalar.copy]
-        vector_copies = [nc.vector.tensor_copy, nc.vector.tensor_copy]
+        grouped = {}
 
-        def transpose_early(rows, copies):
-            grouped = transpose_rows(as_loaded(rows), copies)
+        def transpose_next(i, copies):
+            if i < len(order):
+                kind, tile_index = order[i]
+                rows = x_raw[tile_index] if kind == "x" else w_raw[tile_index]
+                grouped[i] = transpose_rows(as_loaded(rows), copies)
+
+        def quantise_next(i):
+            if i < len(order):
+                kind, tile_index = order[i]
+                if kind == "x":
+                    quantise_tokens(tile_index, grouped[i])
+                else:
+                    quantise_weights(tile_index, grouped[i])
+
+        for i in range(FIRST_TILES + LEAD):
+            transpose_next(i, vector_copies if i == 0 else shared_copies)
             keep_clock_up()
-            return grouped
-
-        grouped_w = {}
-        for n in range(W_TILES):
-            grouped_w[n] = transpose_early(w_raw[n], vector_copies if n == 0 else shared_copies)
-            if n > 0:
-                quantise_weights(n - 1, grouped_w[n - 1])
-        grouped_x = {}
-        for m in range(AHEAD):
-            grouped_x[m] = transpose_rows(as_loaded(x_raw[m]), shared_copies)
-            if m == 0:
-                quantise_weights(W_TILES - 1, grouped_w[W_TILES - 1])
-            else:
-                quantise_tokens(m - 1, grouped_x[m - 1])
+            if i > 0:
+                quantise_next(i - 1)
 
         gain_bank = psum_t.tile([P, LATENT], F32, tag="bank")
         nc.tensor.matmul(out=gain_bank[:], lhsT=ones[:], rhs=gain_rows[:], start=True, stop=True)
         gain = const.tile([P, LATENT], F32)
-        nc.vector.tensor_copy(out=gain[:], in_=gain_bank[:])
+        nc.scalar.copy(out=gain[:], in_=gain_bank[:])
 
+        steps = W_TILES + X_TILES - FIRST_TILES
         latent = {}
-        inverse_rms = {}
-        raw_keys = None
-        for m in range(X_TILES + 1):
-            if m < X_TILES:
+        raw_keys = {}
+        rotation = {}
+        for m in range(FIRST_TILES):
+            latent[m] = psum_lat.tile([P, LATENT], F32, name="latent")
+        for step in range(steps + 2):
+            if step < W_TILES:
+                columns = slice(step * P, (step + 1) * P)
+                if step * P == LATENT:
+                    raw_keys[0] = psum_rope.tile([P, 2, ROPE], F32, name="raw_keys")
+                for m in range(FIRST_TILES):
+                    out = latent[m][:, columns] if step * P < LATENT else raw_keys[0][:, m, :]
+                    multiply(m, out, columns)
+            elif step < steps:
+                m = step - W_TILES + FIRST_TILES
                 latent[m] = psum_lat.tile([P, LATENT], F32, name="latent")
                 multiply(m, latent[m][:], slice(0, LATENT))
                 if m % 2 == 0:
-                    raw_keys = psum_rope.tile([P, 2, ROPE], F32)
-                multiply(m, raw_keys[:, m % 2, :], slice(LATENT, LATENT + ROPE))
-            if m > 0:
-                inverse_rms[m - 1] = inverse_root_mean_square(latent[m - 1])
-            if m + AHEAD < X_TILES:
-                grouped_x[m + AHEAD] = transpose_rows(
-                    as_loaded(x_raw[m + AHEAD]), scalar_copies
-                )
-            if m + AHEAD - 1 < X_TILES:
-                quantise_tokens(m + AHEAD - 1, grouped_x[m + AHEAD - 1])
-            if m > 0:
-                normalise(m - 1, latent[m - 1], inverse_rms[m - 1])
-            if m % 2 == 1:
-                with_cos, with_sin = rotation_products((m - 1) % SEQ_TILES, raw_keys)
-            if m % 2 == 0 and m > 0:
-                rotation_sum(m - 2, with_cos, with_sin)
+                    raw_keys[m // 2] = psum_rope.tile([P, 2, ROPE], F32, name="raw_keys")
+                multiply(m, raw_keys[m // 2][:, m % 2, :], slice(LATENT, LATENT + ROPE))
+
+            done = step - W_TILES + 1
+            if 0 <= done < X_TILES:
+                inverse_rms = inverse_root_mean_square(latent[done])
+            transpose_next(
+                step + FIRST_TILES + LEAD, shared_copies if step < 2 else scalar_copies
+            )
+            quantise_next(step + FIRST_TILES + LEAD - 1)
+            pair, odd = divmod(step - W_TILES, 2)
+            if odd == 0 and 0 <= pair < X_TILES // 2:
+                rotation[pair] = rotation_products(2 * pair % SEQ_TILES, raw_keys[pair])
+            if 0 <= done < X_TILES:
+                normalise(done, latent[done], inverse_rms)
+            if odd == 1 and 0 <= pair < X_TILES // 2:
+                rotation_sum(2 * pair, *rotation[pair])

@@ -56,11 +56,14 @@ def tile_simplemla_pa_kernel(tc, x, wkv_a, kv_norm_w, out_0, out_1):
         tc.tile_pool(name="stage", bufs=4) as stage,
         tc.tile_pool(name="quant", bufs=1) as quant,
         tc.tile_pool(name="work", bufs=3) as work,
-        tc.psum_pool(name="psum_t", bufs=4) as psum_t,
+        tc.psum_pool(name="psum_t", bufs=3) as psum_t,
         tc.psum_pool(name="psum_lat", bufs=3) as psum_lat,
-        tc.psum_pool(name="psum_rope", bufs=1) as psum_rope,
+        tc.psum_pool(name="psum_rope", bufs=2) as psum_rope,
         tc.manual_schedule(),
     ):
+        gain_rows = const.tile([P, LATENT], BF16)
+        nc.gpsimd.memset(gain_rows[:].bitcast(U32), 0)
+
 
         def load_rows(rows, name):
             tile_of_rows = raw.tile([P, DIM], BF16, name=name)
@@ -70,6 +73,10 @@ def tile_simplemla_pa_kernel(tc, x, wkv_a, kv_norm_w, out_0, out_1):
         x_raw = {}
         for m in range(FIRST_TILES):
             x_raw[m] = load_rows(x_rows[m * P : (m + 1) * P, :], "x_raw%d" % m)
+            if m == 0:
+                nc.sync.dma_start(
+                    out=gain_rows[0:1, :], in_=kv_norm_w.rearrange("(o c) -> o c", o=1)
+                )
         w_raw = {}
         for n in range(W_TILES):
             w_raw[n] = load_rows(wkv_a[n * P : (n + 1) * P, :], "w_raw%d" % n)
@@ -84,14 +91,12 @@ def tile_simplemla_pa_kernel(tc, x, wkv_a, kv_norm_w, out_0, out_1):
             channel_multiplier=1,
             allow_small_or_imprecise_dtypes=True,
         )
+        ones = const.tile([P, P], BF16)
+        nc.gpsimd.memset(ones[:], 1.0)
+        zeros = const.tile([P, LATENT], BF16)
+        nc.gpsimd.memset(zeros[:].bitcast(U32), 0)
         identity = const.tile([P, P], F32)
         make_identity(nc, identity[:])
-        gain_rows = const.tile([P, LATENT], BF16)
-        nc.gpsimd.memset(gain_rows[:], 0.0)
-        ones = const.tile([P, P], BF16)
-        nc.vector.memset(ones[:], 1.0)
-        zeros = const.tile([P, LATENT], BF16)
-        nc.vector.memset(zeros[:], 0.0)
         eps = const.tile([P, 1], F32)
         nc.vector.memset(eps[:], EPS)
 
@@ -169,16 +174,22 @@ def tile_simplemla_pa_kernel(tc, x, wkv_a, kv_norm_w, out_0, out_1):
             func=ACT.Sin,
             scale=TWO_PI,
         )
-        cos_pairs = const.tile([P, SEQ_TILES, PAIRS, 2], F32)
+        cos_table = const.tile([P, SEQ_TILES, PAIRS], F32)
         nc.scalar.activation(
-            out=cos_pairs[:].rearrange("p t j e -> p (t j) e"),
-            in_=minus_size[:].unsqueeze(2).to_broadcast([P, SEQ_TILES * PAIRS, 2]),
+            out=cos_table[:].rearrange("p t j -> p (t j)"),
+            in_=minus_size[:],
             func=ACT.Sin,
             scale=TWO_PI,
             bias=half_pi[:, 0:1],
         )
-        nc.scalar.activation(out=table_warmer[:], in_=eps[:], func=ACT.Abs_reciprocal_sqrt)
-        nc.scalar.dma_start(out=gain_rows[0:1, :], in_=kv_norm_w.rearrange("(o c) -> o c", o=1))
+
+        def sort_words(rows):
+            ordered = stage.tile([P, PASSES, 2, P], F32)
+            nc.vector.tensor_copy(
+                out=ordered[:],
+                in_=rows[:].bitcast(F32).rearrange("p (g q u) -> p g u q", g=PASSES, u=2),
+            )
+            return ordered
 
         def transpose_rows(blocks, copies):
             grouped = stage.tile([P, PASSES * P * 4], BF16, align_bytes=64)
@@ -197,6 +208,9 @@ def tile_simplemla_pa_kernel(tc, x, wkv_a, kv_norm_w, out_0, out_1):
                     in_=bank[:].rearrange("p g u r -> p g r u"),
                 )
             return grouped
+
+        def as_sorted(ordered):
+            return lambda g, u: ordered[:, g, u, :]
 
         def as_loaded(rows):
             words = rows[:].bitcast(F32).rearrange("p (g q u) -> p g u q", g=PASSES, u=2)
@@ -270,7 +284,10 @@ def tile_simplemla_pa_kernel(tc, x, wkv_a, kv_norm_w, out_0, out_1):
             nc.vector.tensor_tensor(
                 out=with_cos[:],
                 in0=pairs,
-                in1=cos_pairs[:, t : t + 2].rearrange("p t j e -> p (t j) e"),
+                in1=cos_table[:, t : t + 2]
+                .rearrange("p t j -> p (t j)")
+                .unsqueeze(2)
+                .to_broadcast([P, 2 * PAIRS, 2]),
                 op=ALU.mult,
             )
             with_sin = work.tile([P, 2, 2 * PAIRS], F32)
@@ -305,11 +322,20 @@ def tile_simplemla_pa_kernel(tc, x, wkv_a, kv_norm_w, out_0, out_1):
         scalar_copies = [nc.scalar.copy, nc.scalar.copy]
         grouped = {}
 
+        sorted_words = {}
+
+        def rows_of(i):
+            kind, tile_index = order[i]
+            return x_raw[tile_index] if kind == "x" else w_raw[tile_index]
+
+        def sort_next(i):
+            if i < len(order):
+                sorted_words[i] = sort_words(rows_of(i))
+
         def transpose_next(i, copies):
             if i < len(order):
-                kind, tile_index = order[i]
-                rows = x_raw[tile_index] if kind == "x" else w_raw[tile_index]
-                grouped[i] = transpose_rows(as_loaded(rows), copies)
+                blocks = as_sorted(sorted_words[i]) if i in sorted_words else as_loaded(rows_of(i))
+                grouped[i] = transpose_rows(blocks, copies)
 
         def quantise_next(i):
             if i < len(order):
@@ -319,11 +345,14 @@ def tile_simplemla_pa_kernel(tc, x, wkv_a, kv_norm_w, out_0, out_1):
                 else:
                     quantise_weights(tile_index, grouped[i])
 
+        early_copies = [vector_copies, shared_copies, scalar_copies, shared_copies, scalar_copies]
         for i in range(FIRST_TILES + LEAD):
-            transpose_next(i, vector_copies if i == 0 else shared_copies)
+            transpose_next(i, early_copies[i])
             keep_clock_up()
             if i > 0:
                 quantise_next(i - 1)
+
+        nc.scalar.activation(out=table_warmer[:], in_=eps[:], func=ACT.Abs_reciprocal_sqrt)
 
         gain_bank = psum_t.tile([P, LATENT], F32, tag="bank")
         nc.tensor.matmul(out=gain_bank[:], lhsT=ones[:], rhs=gain_rows[:], start=True, stop=True)
@@ -355,10 +384,10 @@ def tile_simplemla_pa_kernel(tc, x, wkv_a, kv_norm_w, out_0, out_1):
             done = step - W_TILES + 1
             if 0 <= done < X_TILES:
                 inverse_rms = inverse_root_mean_square(latent[done])
-            transpose_next(
-                step + FIRST_TILES + LEAD, shared_copies if step < 2 else scalar_copies
-            )
+            transpose_next(step + FIRST_TILES + LEAD, scalar_copies)
             quantise_next(step + FIRST_TILES + LEAD - 1)
+            if step < W_TILES:
+                sort_next(step + FIRST_TILES + LEAD + 2)
             pair, odd = divmod(step - W_TILES, 2)
             if odd == 0 and 0 <= pair < X_TILES // 2:
                 rotation[pair] = rotation_products(2 * pair % SEQ_TILES, raw_keys[pair])

@@ -33,6 +33,8 @@ BANKS_PER_TILE = WORDS // P // BLOCKS_PER_BANK
 X_TILES = BATCH * SEQ // P
 SEQ_TILES = SEQ // P
 W_TILES = (LATENT + ROPE) // P
+UNIT_ROWS = 2 * P
+UNIT_DEPTH = DIM // 2
 
 FIRST_TILES = 2
 LEAD = 3
@@ -56,30 +58,45 @@ def tile_simplemla_pa_kernel(tc, x, wkv_a, kv_norm_w, out_0, out_1):
         tc.tile_pool(name="stage", bufs=4) as stage,
         tc.tile_pool(name="quant", bufs=1) as quant,
         tc.tile_pool(name="work", bufs=3) as work,
-        tc.psum_pool(name="psum_t", bufs=3) as psum_t,
+        tc.psum_pool(name="psum_t", bufs=4) as psum_t,
         tc.psum_pool(name="psum_lat", bufs=3) as psum_lat,
-        tc.psum_pool(name="psum_rope", bufs=2) as psum_rope,
+        tc.psum_pool(name="psum_rope", bufs=1) as psum_rope,
         tc.manual_schedule(),
     ):
         gain_rows = const.tile([P, LATENT], BF16)
         nc.gpsimd.memset(gain_rows[:].bitcast(U32), 0)
 
 
-        def load_rows(rows, name):
+        def load_rows(rows, name, pieces=1):
             tile_of_rows = raw.tile([P, DIM], BF16, name=name)
-            nc.sync.dma_start(out=tile_of_rows[:], in_=rows)
+            for piece in range(pieces):
+                columns = slice(piece * DIM // pieces, (piece + 1) * DIM // pieces)
+                nc.sync.dma_start(out=tile_of_rows[:, columns], in_=rows[:, columns])
             return tile_of_rows
 
         x_raw = {}
         for m in range(FIRST_TILES):
-            x_raw[m] = load_rows(x_rows[m * P : (m + 1) * P, :], "x_raw%d" % m)
+            x_raw[m] = load_rows(
+                x_rows[m * P : (m + 1) * P, :], "x_raw%d" % m, BANKS_PER_TILE if m == 0 else 1
+            )
             if m == 0:
                 nc.sync.dma_start(
                     out=gain_rows[0:1, :], in_=kv_norm_w.rearrange("(o c) -> o c", o=1)
                 )
         w_raw = {}
         for n in range(W_TILES):
-            w_raw[n] = load_rows(wkv_a[n * P : (n + 1) * P, :], "w_raw%d" % n)
+            w_raw[n] = raw.tile([P, DIM], BF16, name="w_raw%d" % n)
+            if n < W_TILES - 1:
+                rows, half = divmod(n, 2)
+                nc.sync.dma_start(
+                    out=w_raw[n][:].rearrange("p (a k) -> p a k", a=2),
+                    in_=wkv_a[
+                        rows * UNIT_ROWS : (rows + 1) * UNIT_ROWS,
+                        half * UNIT_DEPTH : (half + 1) * UNIT_DEPTH,
+                    ].rearrange("(a p) k -> p a k", a=2),
+                )
+            else:
+                nc.sync.dma_start(out=w_raw[n][:], in_=wkv_a[LATENT : LATENT + ROPE, :])
         for m in range(FIRST_TILES, X_TILES):
             x_raw[m] = load_rows(x_rows[m * P : (m + 1) * P, :], "x_raw%d" % m)
 
@@ -184,47 +201,52 @@ def tile_simplemla_pa_kernel(tc, x, wkv_a, kv_norm_w, out_0, out_1):
         )
 
         def sort_words(rows):
-            ordered = stage.tile([P, PASSES, 2, P], F32)
+            ordered = stage.tile([P, BANKS_PER_TILE, 2, 2, P], F32)
             nc.vector.tensor_copy(
-                out=ordered[:],
-                in_=rows[:].bitcast(F32).rearrange("p (g q u) -> p g u q", g=PASSES, u=2),
+                out=ordered[:].rearrange("p h g u q -> p (h g) u q"),
+                in_=rows[:].bitcast(F32).rearrange("p (c q u) -> p c u q", q=P, u=2),
             )
             return ordered
 
-        def transpose_rows(blocks, copies):
+        def transpose_rows(blocks, layout, copies):
             grouped = stage.tile([P, PASSES * P * 4], BF16, align_bytes=64)
             grouped_words = grouped[:].bitcast(F32).rearrange(
-                "p (g r u) -> p g r u", g=PASSES, u=2
+                layout, h=BANKS_PER_TILE, g=2, u=2
             )
             for h in range(BANKS_PER_TILE):
                 bank = psum_t.tile([P, 2, 2, P], F32, tag="bank")
                 for g in range(2):
                     for u in range(2):
-                        nc.tensor.transpose(
-                            bank[:, g, u, :], blocks(2 * h + g, u), identity[:]
-                        )
+                        nc.tensor.transpose(bank[:, g, u, :], blocks(h, g, u), identity[:])
                 copies[h](
-                    out=grouped_words[:, 2 * h : 2 * h + 2],
+                    out=grouped_words[:, h],
                     in_=bank[:].rearrange("p g u r -> p g r u"),
                 )
             return grouped
 
         def as_sorted(ordered):
-            return lambda g, u: ordered[:, g, u, :]
+            return lambda h, g, u: ordered[:, h, g, u, :]
 
         def as_loaded(rows):
-            words = rows[:].bitcast(F32).rearrange("p (g q u) -> p g u q", g=PASSES, u=2)
-            return lambda g, u: words[:, g, u, :]
+            words = rows[:].bitcast(F32).rearrange(
+                "p (h g q u) -> p h g u q", h=BANKS_PER_TILE, g=2, u=2
+            )
+            return lambda h, g, u: words[:, h, g, u, :]
 
         w_codes = quant.tile([P, PASSES, LATENT + ROPE], U32, align_bytes=64)
         w_scales = quant.tile([P, PASSES, LATENT + ROPE], U8, align_bytes=64)
 
         def quantise_weights(n, grouped):
-            for g in range(PASSES):
+            if n < W_TILES - 1:
+                rows, half = divmod(n, 2)
+                passes, first, count = [2 * half, 2 * half + 1], rows * UNIT_ROWS, UNIT_ROWS
+            else:
+                passes, first, count = list(range(PASSES)), LATENT, ROPE
+            for i, g in enumerate(passes):
                 nc.vector.quantize_mx(
-                    out=w_codes[:, g, n * P : (n + 1) * P].bitcast(FP8X4),
-                    scales=w_scales[:, g, n * P : (n + 1) * P],
-                    in_=grouped[:, g * 4 * P : (g + 1) * 4 * P],
+                    out=w_codes[:, g, first : first + count].bitcast(FP8X4),
+                    scales=w_scales[:, g, first : first + count],
+                    in_=grouped[:, i * 4 * count : (i + 1) * 4 * count],
                 )
 
         x_codes = {}
@@ -237,8 +259,8 @@ def tile_simplemla_pa_kernel(tc, x, wkv_a, kv_norm_w, out_0, out_1):
                 out=x_codes[m][:].bitcast(FP8X4), scales=x_scales[m][:], in_=grouped[:]
             )
 
-        def multiply(m, out, columns):
-            for g in range(PASSES):
+        def multiply(m, out, columns, passes=range(PASSES)):
+            for g in passes:
                 nc.tensor.matmul_mx(
                     out=out,
                     lhsT=x_codes[m][:, g * P : (g + 1) * P].bitcast(FP8X4),
@@ -249,48 +271,48 @@ def tile_simplemla_pa_kernel(tc, x, wkv_a, kv_norm_w, out_0, out_1):
                     stop=(g == PASSES - 1),
                 )
 
-        def inverse_root_mean_square(latent):
+        sum_squares = {}
+        inverse_rms = {}
+
+        def square(m):
             squares = work.tile([P, LATENT], BF16)
-            sum_squares = work.tile([P, 1], F32)
+            sum_squares[m] = work.tile([P, 1], F32, name="sum_squares")
             nc.scalar.activation(
-                out=squares[:], in_=latent[:], func=ACT.Square, accum_out=sum_squares[:]
+                out=squares[:], in_=latent[m][:], func=ACT.Square, accum_out=sum_squares[m][:]
             )
-            inverse_rms = work.tile([P, 1], F32)
+            inverse_rms[m] = work.tile([P, 1], F32, name="inverse_rms")
             nc.scalar.activation(
-                out=inverse_rms[:],
-                in_=sum_squares[:],
+                out=inverse_rms[m][:],
+                in_=sum_squares[m][:],
                 func=ACT.Abs_reciprocal_sqrt,
                 scale=1.0 / LATENT,
                 bias=eps[:, 0:1],
             )
-            return inverse_rms
 
-        def normalise(m, latent, inverse_rms):
+        def normalise(m):
             kv_cache = work.tile([P, LATENT], F32, bufs=4)
             nc.vector.scalar_tensor_tensor(
                 out=kv_cache[:],
-                in0=latent[:],
-                scalar=inverse_rms[:, 0:1],
+                in0=latent[m][:],
+                scalar=inverse_rms[m][:, 0:1],
                 in1=gain[:],
                 op0=ALU.mult,
                 op1=ALU.mult,
             )
             nc.sync.dma_start(out=kv_cache_rows[m * P : (m + 1) * P, :], in_=kv_cache[:])
 
-        def rotation_products(t, raw_keys):
+        def rotation_products(t, count, raw_keys):
             pairs = raw_keys[:].rearrange("p t (j e) -> p (t j) e", e=2)
-            sines = sin_table[:, t : t + 2].rearrange("p t j -> p (t j)")
-            with_cos = work.tile([P, 2 * PAIRS, 2], F32)
+            sines = sin_table[:, t : t + count].rearrange("p t j -> p (t j)")
+            cosines = cos_table[:, t : t + count].rearrange("p t j -> p (t j)")
+            with_cos = work.tile([P, count * PAIRS, 2], F32, name="with_cos%d" % count)
             nc.vector.tensor_tensor(
                 out=with_cos[:],
                 in0=pairs,
-                in1=cos_table[:, t : t + 2]
-                .rearrange("p t j -> p (t j)")
-                .unsqueeze(2)
-                .to_broadcast([P, 2 * PAIRS, 2]),
+                in1=cosines.unsqueeze(2).to_broadcast([P, count * PAIRS, 2]),
                 op=ALU.mult,
             )
-            with_sin = work.tile([P, 2, 2 * PAIRS], F32)
+            with_sin = work.tile([P, 2, count * PAIRS], F32, name="with_sin%d" % count)
             nc.vector.scalar_tensor_tensor(
                 out=with_sin[:, 0, :],
                 in0=pairs[:, :, 1],
@@ -304,20 +326,19 @@ def tile_simplemla_pa_kernel(tc, x, wkv_a, kv_norm_w, out_0, out_1):
             )
             return with_cos, with_sin
 
-        def rotation_sum(m, with_cos, with_sin):
-            k_pe = work.tile([P, 2 * PAIRS, 2], F32)
+        def rotation_sum(m, count, with_cos, with_sin):
+            k_pe = work.tile([P, count * PAIRS, 2], F32, name="k_pe%d" % count)
             nc.vector.tensor_tensor(
                 out=k_pe[:], in0=with_cos[:], in1=with_sin[:].rearrange("p e c -> p c e"), op=ALU.add
             )
             nc.sync.dma_start(
-                out=k_pe_rows[m * P : (m + 2) * P, :].rearrange("(t p) c -> p t c", p=P),
-                in_=k_pe[:].rearrange("p (t j) e -> p t (j e)", t=2),
+                out=k_pe_rows[m * P : (m + count) * P, :].rearrange("(t p) c -> p t c", p=P),
+                in_=k_pe[:].rearrange("p (t j) e -> p t (j e)", t=count),
             )
 
         order = [("x", m) for m in range(FIRST_TILES)]
         order += [("w", n) for n in range(W_TILES)]
         order += [("x", m) for m in range(FIRST_TILES, X_TILES)]
-        vector_copies = [nc.vector.tensor_copy, nc.vector.tensor_copy]
         shared_copies = [nc.vector.tensor_copy, nc.scalar.copy]
         scalar_copies = [nc.scalar.copy, nc.scalar.copy]
         grouped = {}
@@ -335,7 +356,10 @@ def tile_simplemla_pa_kernel(tc, x, wkv_a, kv_norm_w, out_0, out_1):
         def transpose_next(i, copies):
             if i < len(order):
                 blocks = as_sorted(sorted_words[i]) if i in sorted_words else as_loaded(rows_of(i))
-                grouped[i] = transpose_rows(blocks, copies)
+                kind, tile_index = order[i]
+                latent_weights = kind == "w" and tile_index < W_TILES - 1
+                layout = "p (g h r u) -> p h g r u" if latent_weights else "p (h g r u) -> p h g r u"
+                grouped[i] = transpose_rows(blocks, layout, copies)
 
         def quantise_next(i):
             if i < len(order):
@@ -345,7 +369,7 @@ def tile_simplemla_pa_kernel(tc, x, wkv_a, kv_norm_w, out_0, out_1):
                 else:
                     quantise_weights(tile_index, grouped[i])
 
-        early_copies = [vector_copies, shared_copies, scalar_copies, shared_copies, scalar_copies]
+        early_copies = [shared_copies, shared_copies, scalar_copies, scalar_copies, scalar_copies]
         for i in range(FIRST_TILES + LEAD):
             transpose_next(i, early_copies[i])
             keep_clock_up()
@@ -359,39 +383,110 @@ def tile_simplemla_pa_kernel(tc, x, wkv_a, kv_norm_w, out_0, out_1):
         gain = const.tile([P, LATENT], F32)
         nc.scalar.copy(out=gain[:], in_=gain_bank[:])
 
-        steps = W_TILES + X_TILES - FIRST_TILES
         latent = {}
         raw_keys = {}
         rotation = {}
         for m in range(FIRST_TILES):
             latent[m] = psum_lat.tile([P, LATENT], F32, name="latent")
-        for step in range(steps + 2):
-            if step < W_TILES:
-                columns = slice(step * P, (step + 1) * P)
-                if step * P == LATENT:
-                    raw_keys[0] = psum_rope.tile([P, 2, ROPE], F32, name="raw_keys")
-                for m in range(FIRST_TILES):
-                    out = latent[m][:, columns] if step * P < LATENT else raw_keys[0][:, m, :]
-                    multiply(m, out, columns)
-            elif step < steps:
-                m = step - W_TILES + FIRST_TILES
-                latent[m] = psum_lat.tile([P, LATENT], F32, name="latent")
-                multiply(m, latent[m][:], slice(0, LATENT))
-                if m % 2 == 0:
-                    raw_keys[m // 2] = psum_rope.tile([P, 2, ROPE], F32, name="raw_keys")
-                multiply(m, raw_keys[m // 2][:, m % 2, :], slice(LATENT, LATENT + ROPE))
+        together = {0: 4, 4: 2, 6: 2}
+        first_of = {m: start for start in together for m in range(start, start + together[start])}
 
-            done = step - W_TILES + 1
-            if 0 <= done < X_TILES:
-                inverse_rms = inverse_root_mean_square(latent[done])
-            transpose_next(step + FIRST_TILES + LEAD, scalar_copies)
-            quantise_next(step + FIRST_TILES + LEAD - 1)
-            if step < W_TILES:
-                sort_next(step + FIRST_TILES + LEAD + 2)
-            pair, odd = divmod(step - W_TILES, 2)
-            if odd == 0 and 0 <= pair < X_TILES // 2:
-                rotation[pair] = rotation_products(2 * pair % SEQ_TILES, raw_keys[pair])
-            if 0 <= done < X_TILES:
-                normalise(done, latent[done], inverse_rms)
-            if odd == 1 and 0 <= pair < X_TILES // 2:
-                rotation_sum(2 * pair, *rotation[pair])
+        def keys_of(m):
+            start = first_of[m]
+            if start not in raw_keys:
+                pool = psum_t if start == 6 else psum_rope
+                raw_keys[start] = pool.tile(
+                    [P, together[start], ROPE],
+                    F32,
+                    name="raw_keys%d" % start,
+                    tag="bank" if start == 6 else "raw_keys",
+                )
+            return raw_keys[start][:, m - start, :]
+
+        def multiply_weights(n):
+            for m in range(FIRST_TILES):
+                if n < W_TILES - 1:
+                    rows, half = divmod(n, 2)
+                    columns = slice(rows * UNIT_ROWS, (rows + 1) * UNIT_ROWS)
+                    multiply(m, latent[m][:, columns], columns, [2 * half, 2 * half + 1])
+                else:
+                    multiply(m, keys_of(m), slice(LATENT, LATENT + ROPE))
+
+        def multiply_tokens(m):
+            if m < X_TILES - 3:
+                latent[m] = psum_lat.tile([P, LATENT], F32, name="latent")
+            else:
+                latent[m] = psum_t.tile([P, LATENT], F32, name="late_latent", tag="bank")
+            multiply(m, latent[m][:], slice(0, LATENT))
+            multiply(m, keys_of(m), slice(LATENT, LATENT + ROPE))
+
+        def rotate(start):
+            rotation[start] = rotation_products(
+                start % SEQ_TILES, together[start], raw_keys[start]
+            )
+
+        def finish_rotation(start):
+            rotation_sum(start, together[start], *rotation[start])
+
+        multiply_weights(0)
+        multiply_weights(1)
+        quantise_next(4)
+        transpose_next(5, shared_copies)
+        quantise_next(5)
+        sort_next(7)
+        transpose_next(6, scalar_copies)
+        sort_next(8)
+
+        multiply_weights(2)
+        multiply_weights(3)
+        quantise_next(6)
+        transpose_next(7, scalar_copies)
+        sort_next(9)
+        transpose_next(8, scalar_copies)
+        sort_next(10)
+        quantise_next(7)
+        square(0)
+        square(1)
+
+        multiply_weights(4)
+        transpose_next(9, scalar_copies)
+        quantise_next(8)
+        transpose_next(10, scalar_copies)
+        normalise(0)
+        sort_next(11)
+        normalise(1)
+
+        multiply_tokens(2)
+        multiply_tokens(3)
+        quantise_next(9)
+        square(2)
+        transpose_next(11, scalar_copies)
+        square(3)
+        rotate(0)
+        quantise_next(10)
+        transpose_next(12, scalar_copies)
+        normalise(2)
+        quantise_next(11)
+
+        multiply_tokens(4)
+        square(4)
+        normalise(3)
+        quantise_next(12)
+        finish_rotation(0)
+
+        multiply_tokens(5)
+        square(5)
+        normalise(4)
+        rotate(4)
+
+        multiply_tokens(6)
+        square(6)
+        normalise(5)
+        finish_rotation(4)
+
+        multiply_tokens(7)
+        square(7)
+        normalise(6)
+        rotate(6)
+        normalise(7)
+        finish_rotation(6)

@@ -372,7 +372,6 @@ def tile_simplemla_pa_kernel(tc, x, wkv_a, kv_norm_w, out_0, out_1):
         early_copies = [shared_copies, shared_copies, scalar_copies, scalar_copies, scalar_copies]
         for i in range(FIRST_TILES + LEAD):
             transpose_next(i, early_copies[i])
-            keep_clock_up()
             if i > 0:
                 quantise_next(i - 1)
 
@@ -388,18 +387,18 @@ def tile_simplemla_pa_kernel(tc, x, wkv_a, kv_norm_w, out_0, out_1):
         rotation = {}
         for m in range(FIRST_TILES):
             latent[m] = psum_lat.tile([P, LATENT], F32, name="latent")
-        together = {0: 4, 4: 2, 6: 2}
+        together = {0: 4, 4: 2, 6: 1, 7: 1}
         first_of = {m: start for start in together for m in range(start, start + together[start])}
 
         def keys_of(m):
             start = first_of[m]
             if start not in raw_keys:
-                pool = psum_t if start == 6 else psum_rope
+                pool = psum_t if start >= 6 else psum_rope
                 raw_keys[start] = pool.tile(
                     [P, together[start], ROPE],
                     F32,
                     name="raw_keys%d" % start,
-                    tag="bank" if start == 6 else "raw_keys",
+                    tag="bank" if start >= 6 else "raw_keys",
                 )
             return raw_keys[start][:, m - start, :]
 
@@ -413,12 +412,63 @@ def tile_simplemla_pa_kernel(tc, x, wkv_a, kv_norm_w, out_0, out_1):
                     multiply(m, keys_of(m), slice(LATENT, LATENT + ROPE))
 
         def multiply_tokens(m):
-            if m < X_TILES - 3:
-                latent[m] = psum_lat.tile([P, LATENT], F32, name="latent")
-            else:
+            if m in (5, 6):
                 latent[m] = psum_t.tile([P, LATENT], F32, name="late_latent", tag="bank")
+            else:
+                latent[m] = psum_lat.tile([P, LATENT], F32, name="latent")
             multiply(m, latent[m][:], slice(0, LATENT))
             multiply(m, keys_of(m), slice(LATENT, LATENT + ROPE))
+
+        HALF = LATENT // 2
+        last = X_TILES - 1
+        half_banks = []
+
+        def multiply_last():
+            for half in range(2):
+                bank = psum_lat.tile([P, LATENT], F32, name="half_bank", tag="latent")
+                half_banks.append(bank)
+                columns = slice(half * HALF, (half + 1) * HALF)
+                multiply(last, bank[:, 0:HALF], columns)
+            multiply(last, keys_of(last), slice(LATENT, LATENT + ROPE))
+
+        def square_last():
+            so_far = eps
+            for half in range(2):
+                squares = work.tile([P, LATENT], BF16)
+                half_sum = work.tile([P, 1], F32)
+                nc.scalar.activation(
+                    out=squares[:, 0:HALF],
+                    in_=half_banks[half][:, 0:HALF],
+                    func=ACT.Square,
+                    accum_out=half_sum[:],
+                )
+                total = work.tile([P, 1], F32)
+                nc.scalar.activation(
+                    out=total[:],
+                    in_=half_sum[:],
+                    func=ACT.Identity if half == 0 else ACT.Abs_reciprocal_sqrt,
+                    scale=1.0 / LATENT,
+                    bias=so_far[:, 0:1],
+                )
+                so_far = total
+            inverse_rms[last] = so_far
+
+        def normalise_last():
+            queues = [nc.sync, nc.scalar]
+            for half in range(2):
+                columns = slice(half * HALF, (half + 1) * HALF)
+                kv_half = work.tile([P, HALF], F32, bufs=2)
+                nc.vector.scalar_tensor_tensor(
+                    out=kv_half[:],
+                    in0=half_banks[half][:, 0:HALF],
+                    scalar=inverse_rms[last][:, 0:1],
+                    in1=gain[:, columns],
+                    op0=ALU.mult,
+                    op1=ALU.mult,
+                )
+                queues[half].dma_start(
+                    out=kv_cache_rows[last * P : (last + 1) * P, columns], in_=kv_half[:]
+                )
 
         def rotate(start):
             rotation[start] = rotation_products(
@@ -484,9 +534,11 @@ def tile_simplemla_pa_kernel(tc, x, wkv_a, kv_norm_w, out_0, out_1):
         normalise(5)
         finish_rotation(4)
 
-        multiply_tokens(7)
-        square(7)
-        normalise(6)
+        multiply_last()
+        square_last()
         rotate(6)
-        normalise(7)
+        normalise(6)
         finish_rotation(6)
+        rotate(7)
+        normalise_last()
+        finish_rotation(7)

@@ -152,53 +152,62 @@ def tile_simplemla_pa_kernel(tc, x, wkv_a, kv_norm_w, out_0, out_1):
             op0=ALU.mult,
             op1=ALU.mult,
         )
-        turns = const.tile([P, SEQ_TILES * PAIRS], F32)
-        nc.vector.tensor_tensor(
-            out=turns[:].rearrange("p (c b) -> p c b", b=STEPS),
-            in0=coarse_turns[:]
-            .rearrange("p t a -> p (t a)")
-            .unsqueeze(2)
-            .to_broadcast([P, SEQ_TILES * STEPS, STEPS]),
-            in1=powers[:, 1, :].unsqueeze(1).to_broadcast([P, SEQ_TILES * STEPS, STEPS]),
-            op=ALU.mult,
-        )
-        whole_turns = const.tile([P, SEQ_TILES * PAIRS], F32)
-        nc.vector.tensor_scalar(
-            out=whole_turns[:],
-            in0=turns[:],
-            scalar1=ROUND_MAGIC,
-            scalar2=ROUND_MAGIC,
-            op0=ALU.add,
-            op1=ALU.subtract,
-        )
-        part_turns = const.tile([P, SEQ_TILES * PAIRS], F32)
-        nc.vector.tensor_tensor(
-            out=part_turns[:], in0=turns[:], in1=whole_turns[:], op=ALU.subtract
-        )
-        minus_size = const.tile([P, SEQ_TILES * PAIRS], F32)
-        nc.vector.scalar_tensor_tensor(
-            out=minus_size[:],
-            in0=part_turns[:],
-            scalar=-1.0,
-            in1=part_turns[:],
-            op0=ALU.mult,
-            op1=ALU.min,
-        )
+        wide = [P, SEQ_TILES * PAIRS]
+        turns = const.tile(wide, F32)
+        whole_turns = const.tile(wide, F32)
+        part_turns = const.tile(wide, F32)
+        minus_size = const.tile(wide, F32)
         sin_table = const.tile([P, SEQ_TILES, PAIRS], F32)
-        nc.scalar.activation(
-            out=sin_table[:].rearrange("p t j -> p (t j)"),
-            in_=part_turns[:],
-            func=ACT.Sin,
-            scale=TWO_PI,
-        )
         cos_table = const.tile([P, SEQ_TILES, PAIRS], F32)
-        nc.scalar.activation(
-            out=cos_table[:].rearrange("p t j -> p (t j)"),
-            in_=minus_size[:],
-            func=ACT.Sin,
-            scale=TWO_PI,
-            bias=half_pi[:, 0:1],
-        )
+
+        def table_step(i):
+            if i == 0:
+                nc.vector.tensor_tensor(
+                    out=turns[:].rearrange("p (c b) -> p c b", b=STEPS),
+                    in0=coarse_turns[:]
+                    .rearrange("p t a -> p (t a)")
+                    .unsqueeze(2)
+                    .to_broadcast([P, SEQ_TILES * STEPS, STEPS]),
+                    in1=powers[:, 1, :].unsqueeze(1).to_broadcast([P, SEQ_TILES * STEPS, STEPS]),
+                    op=ALU.mult,
+                )
+            elif i == 1:
+                nc.vector.tensor_scalar(
+                    out=whole_turns[:],
+                    in0=turns[:],
+                    scalar1=ROUND_MAGIC,
+                    scalar2=ROUND_MAGIC,
+                    op0=ALU.add,
+                    op1=ALU.subtract,
+                )
+            elif i == 2:
+                nc.vector.tensor_tensor(
+                    out=part_turns[:], in0=turns[:], in1=whole_turns[:], op=ALU.subtract
+                )
+            elif i == 3:
+                nc.vector.scalar_tensor_tensor(
+                    out=minus_size[:],
+                    in0=part_turns[:],
+                    scalar=-1.0,
+                    in1=part_turns[:],
+                    op0=ALU.mult,
+                    op1=ALU.min,
+                )
+
+        def sines():
+            nc.scalar.activation(
+                out=sin_table[:].rearrange("p t j -> p (t j)"),
+                in_=part_turns[:],
+                func=ACT.Sin,
+                scale=TWO_PI,
+            )
+            nc.scalar.activation(
+                out=cos_table[:].rearrange("p t j -> p (t j)"),
+                in_=minus_size[:],
+                func=ACT.Sin,
+                scale=TWO_PI,
+                bias=half_pi[:, 0:1],
+            )
 
         def sort_words(rows):
             ordered = stage.tile([P, BANKS_PER_TILE, 2, 2, P], F32)
@@ -341,6 +350,7 @@ def tile_simplemla_pa_kernel(tc, x, wkv_a, kv_norm_w, out_0, out_1):
         order += [("x", m) for m in range(FIRST_TILES, X_TILES)]
         shared_copies = [nc.vector.tensor_copy, nc.scalar.copy]
         scalar_copies = [nc.scalar.copy, nc.scalar.copy]
+        vector_copies = [nc.vector.tensor_copy, nc.vector.tensor_copy]
         grouped = {}
 
         sorted_words = {}
@@ -374,7 +384,9 @@ def tile_simplemla_pa_kernel(tc, x, wkv_a, kv_norm_w, out_0, out_1):
             transpose_next(i, early_copies[i])
             if i > 0:
                 quantise_next(i - 1)
+            table_step(i)
 
+        sines()
         nc.scalar.activation(out=table_warmer[:], in_=eps[:], func=ACT.Abs_reciprocal_sqrt)
 
         gain_bank = psum_t.tile([P, LATENT], F32, tag="bank")
@@ -481,7 +493,7 @@ def tile_simplemla_pa_kernel(tc, x, wkv_a, kv_norm_w, out_0, out_1):
         multiply_weights(0)
         multiply_weights(1)
         quantise_next(4)
-        transpose_next(5, shared_copies)
+        transpose_next(5, vector_copies)
         quantise_next(5)
         sort_next(7)
         transpose_next(6, scalar_copies)

@@ -38,7 +38,6 @@ UNIT_DEPTH = DIM // 2
 
 FIRST_TILES = 2
 LEAD = 3
-WARM_UP = 3
 
 TWO_PI = 2.0 * math.pi
 ROUND_MAGIC = 1.5 * 2.0**23
@@ -63,10 +62,6 @@ def tile_simplemla_pa_kernel(tc, x, wkv_a, kv_norm_w, out_0, out_1):
         tc.psum_pool(name="psum_rope", bufs=1) as psum_rope,
         tc.manual_schedule(),
     ):
-        gain_rows = const.tile([P, LATENT], BF16)
-        nc.gpsimd.memset(gain_rows[:].bitcast(U32), 0)
-
-
         def load_rows(rows, name, pieces=1):
             tile_of_rows = raw.tile([P, DIM], BF16, name=name)
             for piece in range(pieces):
@@ -79,10 +74,6 @@ def tile_simplemla_pa_kernel(tc, x, wkv_a, kv_norm_w, out_0, out_1):
             x_raw[m] = load_rows(
                 x_rows[m * P : (m + 1) * P, :], "x_raw%d" % m, BANKS_PER_TILE if m == 0 else 1
             )
-            if m == 0:
-                nc.sync.dma_start(
-                    out=gain_rows[0:1, :], in_=kv_norm_w.rearrange("(o c) -> o c", o=1)
-                )
         w_raw = {}
         for n in range(W_TILES):
             w_raw[n] = raw.tile([P, DIM], BF16, name="w_raw%d" % n)
@@ -97,7 +88,10 @@ def tile_simplemla_pa_kernel(tc, x, wkv_a, kv_norm_w, out_0, out_1):
                 )
             else:
                 nc.sync.dma_start(out=w_raw[n][:], in_=wkv_a[LATENT : LATENT + ROPE, :])
+        gain = const.tile([P, LATENT], BF16)
         for m in range(FIRST_TILES, X_TILES):
+            if m == X_TILES - 2:
+                nc.sync.dma_start(out=gain[:], in_=kv_norm_w.partition_broadcast(P))
             x_raw[m] = load_rows(x_rows[m * P : (m + 1) * P, :], "x_raw%d" % m)
 
         position = const.tile([P, SEQ_TILES], F32)
@@ -108,22 +102,10 @@ def tile_simplemla_pa_kernel(tc, x, wkv_a, kv_norm_w, out_0, out_1):
             channel_multiplier=1,
             allow_small_or_imprecise_dtypes=True,
         )
-        ones = const.tile([P, P], BF16)
-        nc.gpsimd.memset(ones[:], 1.0)
-        zeros = const.tile([P, LATENT], BF16)
-        nc.gpsimd.memset(zeros[:].bitcast(U32), 0)
         identity = const.tile([P, P], F32)
         make_identity(nc, identity[:])
         eps = const.tile([P, 1], F32)
         nc.vector.memset(eps[:], EPS)
-
-        idle_bank = psum_lat.tile([P, LATENT], F32, name="latent")
-
-        def keep_clock_up():
-            nc.tensor.matmul(out=idle_bank[:], lhsT=ones[:], rhs=zeros[:], start=True, stop=True)
-
-        for warm in range(WARM_UP):
-            keep_clock_up()
 
         table_warmer = const.tile([P, 1], F32)
         nc.scalar.activation(out=table_warmer[:], in_=eps[:], func=ACT.Sin)
@@ -389,11 +371,6 @@ def tile_simplemla_pa_kernel(tc, x, wkv_a, kv_norm_w, out_0, out_1):
         sines()
         nc.scalar.activation(out=table_warmer[:], in_=eps[:], func=ACT.Abs_reciprocal_sqrt)
 
-        gain_bank = psum_t.tile([P, LATENT], F32, tag="bank")
-        nc.tensor.matmul(out=gain_bank[:], lhsT=ones[:], rhs=gain_rows[:], start=True, stop=True)
-        gain = const.tile([P, LATENT], F32)
-        nc.scalar.copy(out=gain[:], in_=gain_bank[:])
-
         latent = {}
         raw_keys = {}
         rotation = {}
@@ -444,7 +421,6 @@ def tile_simplemla_pa_kernel(tc, x, wkv_a, kv_norm_w, out_0, out_1):
             multiply(last, keys_of(last), slice(LATENT, LATENT + ROPE))
 
         def square_last():
-            so_far = eps
             for half in range(2):
                 squares = work.tile([P, LATENT], BF16)
                 half_sum = work.tile([P, 1], F32)
@@ -454,16 +430,24 @@ def tile_simplemla_pa_kernel(tc, x, wkv_a, kv_norm_w, out_0, out_1):
                     func=ACT.Square,
                     accum_out=half_sum[:],
                 )
-                total = work.tile([P, 1], F32)
-                nc.scalar.activation(
-                    out=total[:],
-                    in_=half_sum[:],
-                    func=ACT.Identity if half == 0 else ACT.Abs_reciprocal_sqrt,
-                    scale=1.0 / LATENT,
-                    bias=so_far[:, 0:1],
-                )
-                so_far = total
-            inverse_rms[last] = so_far
+                if half == 0:
+                    share = work.tile([P, 1], F32)
+                    nc.gpsimd.tensor_scalar(
+                        out=share[:],
+                        in0=half_sum[:],
+                        scalar1=1.0 / LATENT,
+                        scalar2=EPS,
+                        op0=ALU.mult,
+                        op1=ALU.add,
+                    )
+            inverse_rms[last] = work.tile([P, 1], F32, name="inverse_rms")
+            nc.scalar.activation(
+                out=inverse_rms[last][:],
+                in_=half_sum[:],
+                func=ACT.Abs_reciprocal_sqrt,
+                scale=1.0 / LATENT,
+                bias=share[:, 0:1],
+            )
 
         def normalise_last():
             queues = [nc.sync, nc.scalar]
@@ -491,25 +475,23 @@ def tile_simplemla_pa_kernel(tc, x, wkv_a, kv_norm_w, out_0, out_1):
             rotation_sum(start, together[start], *rotation[start])
 
         multiply_weights(0)
-        multiply_weights(1)
         quantise_next(4)
-        transpose_next(5, vector_copies)
-        quantise_next(5)
+        transpose_next(5, shared_copies)
         sort_next(7)
+        multiply_weights(1)
+        quantise_next(5)
         transpose_next(6, scalar_copies)
         sort_next(8)
-
         multiply_weights(2)
-        multiply_weights(3)
-        quantise_next(6)
         transpose_next(7, scalar_copies)
+        quantise_next(6)
         sort_next(9)
+        multiply_weights(3)
         transpose_next(8, scalar_copies)
         sort_next(10)
         quantise_next(7)
         square(0)
         square(1)
-
         multiply_weights(4)
         transpose_next(9, scalar_copies)
         quantise_next(8)
@@ -517,7 +499,6 @@ def tile_simplemla_pa_kernel(tc, x, wkv_a, kv_norm_w, out_0, out_1):
         normalise(0)
         sort_next(11)
         normalise(1)
-
         multiply_tokens(2)
         multiply_tokens(3)
         quantise_next(9)
@@ -529,28 +510,24 @@ def tile_simplemla_pa_kernel(tc, x, wkv_a, kv_norm_w, out_0, out_1):
         transpose_next(12, scalar_copies)
         normalise(2)
         quantise_next(11)
-
         multiply_tokens(4)
         square(4)
         normalise(3)
         quantise_next(12)
         finish_rotation(0)
-
         multiply_tokens(5)
         square(5)
         normalise(4)
         rotate(4)
-
         multiply_tokens(6)
         square(6)
         normalise(5)
         finish_rotation(4)
-
         multiply_last()
         square_last()
         rotate(6)
         normalise(6)
-        finish_rotation(6)
         rotate(7)
         normalise_last()
+        finish_rotation(6)
         finish_rotation(7)

import math

import concourse.mybir as mybir
from concourse.masks import make_identity

F32 = mybir.dt.float32
BF16 = mybir.dt.bfloat16
I32 = mybir.dt.int32
U32 = mybir.dt.uint32
U8 = mybir.dt.uint8
FP8X4 = mybir.dt.float8_e4m3fn_x4
ALU = mybir.AluOpType
ACT = mybir.ActivationFunctionType

P = 128
BATCH = 2
SEQ = 512
DIM = 2048
LATENT = 512
ROPE = 128
PAIRS = ROPE // 2
DOUBLINGS = 3
STEPS = 2**DOUBLINGS
assert STEPS * STEPS == PAIRS
THETA = 10000.0
EPS = 1e-6

K_PASS = 4 * P
PASSES = DIM // K_PASS
WORDS = DIM // 2
BLOCKS_PER_BANK = 4
BANKS_PER_TILE = WORDS // P // BLOCKS_PER_BANK
X_TILES = BATCH * SEQ // P
SEQ_TILES = SEQ // P
W_TILES = (LATENT + ROPE) // P
UNIT_ROWS = 2 * P
UNIT_DEPTH = DIM // 2

FIRST_TILES = 2
LEAD = 3

TWO_PI = 2.0 * math.pi
ROUND_MAGIC = 1.5 * 2.0**23

FLOPS = 2 * BATCH * SEQ * DIM * (LATENT + ROPE)


def tile_simplemla_pa_kernel(tc, x, wkv_a, kv_norm_w, out_0, out_1):
    nc = tc.nc
    x_rows = x.flatten_outer_dims()
    kv_cache_rows = out_0.flatten_outer_dims()
    k_pe_rows = out_1.flatten_outer_dims()

    with (
        tc.tile_pool(name="const", bufs=1) as const,
        tc.tile_pool(name="raw", bufs=1) as raw,
        tc.tile_pool(name="stage", bufs=4) as stage,
        tc.tile_pool(name="quant", bufs=1) as quant,
        tc.tile_pool(name="work", bufs=3) as work,
        tc.psum_pool(name="psum_t", bufs=4) as psum_t,
        tc.psum_pool(name="psum_lat", bufs=3) as psum_lat,
        tc.psum_pool(name="psum_rope", bufs=1) as psum_rope,
        tc.manual_schedule(),
    ):
        def load_rows(rows, name, pieces=1):
            tile_of_rows = raw.tile([P, DIM], BF16, name=name)
            for piece in range(pieces):
                columns = slice(piece * DIM // pieces, (piece + 1) * DIM // pieces)
                nc.sync.dma_start(out=tile_of_rows[:, columns], in_=rows[:, columns])
            return tile_of_rows

        x_raw = {}
        for m in range(FIRST_TILES):
            x_raw[m] = load_rows(
                x_rows[m * P : (m + 1) * P, :], "x_raw%d" % m, BANKS_PER_TILE if m == 0 else 1
            )
        w_raw = {}
        for n in range(W_TILES):
            w_raw[n] = raw.tile([P, DIM], BF16, name="w_raw%d" % n)
            if n < W_TILES - 1:
                rows, half = divmod(n, 2)
                nc.sync.dma_start(
                    out=w_raw[n][:].rearrange("p (a k) -> p a k", a=2),
                    in_=wkv_a[
                        rows * UNIT_ROWS : (rows + 1) * UNIT_ROWS,
                        half * UNIT_DEPTH : (half + 1) * UNIT_DEPTH,
                    ].rearrange("(a p) k -> p a k", a=2),
                )
            else:
                nc.sync.dma_start(out=w_raw[n][:], in_=wkv_a[LATENT : LATENT + ROPE, :])
        gain = const.tile([P, LATENT], BF16)
        for m in range(FIRST_TILES, X_TILES):
            if m == X_TILES - 2:
                nc.sync.dma_start(out=gain[:], in_=kv_norm_w.partition_broadcast(P))
            x_raw[m] = load_rows(x_rows[m * P : (m + 1) * P, :], "x_raw%d" % m)

        position = const.tile([P, SEQ_TILES], F32)
        nc.gpsimd.iota(
            position[:],
            pattern=[[P, SEQ_TILES]],
            base=0,
            channel_multiplier=1,
            allow_small_or_imprecise_dtypes=True,
        )
        identity = const.tile([P, P], F32)
        make_identity(nc, identity[:])
        eps = const.tile([P, 1], F32)
        nc.vector.memset(eps[:], EPS)

        table_warmer = const.tile([P, 1], F32)
        nc.scalar.activation(out=table_warmer[:], in_=eps[:], func=ACT.Sin)
        powers = const.tile([P, 2, STEPS], F32)
        nc.vector.memset(powers[:, :, 0:1], 1.0)
        for doubling in range(DOUBLINGS):
            n = 2**doubling
            for plane, step in ((0, STEPS), (1, 1)):
                nc.vector.tensor_scalar(
                    out=powers[:, plane, n : 2 * n],
                    in0=powers[:, plane, 0:n],
                    scalar1=THETA ** (-n * step / PAIRS),
                    scalar2=None,
                    op0=ALU.mult,
                )
        half_pi = const.tile([P, 1], F32)
        nc.vector.tensor_scalar(
            out=half_pi[:], in0=powers[:, 0, 0:1], scalar1=TWO_PI / 4, scalar2=None, op0=ALU.mult
        )
        coarse_turns = const.tile([P, SEQ_TILES, STEPS], F32)
        nc.vector.scalar_tensor_tensor(
            out=coarse_turns[:],
            in0=powers[:, 0, :].unsqueeze(1).to_broadcast([P, SEQ_TILES, STEPS]),
            scalar=1.0 / TWO_PI,
            in1=position[:].unsqueeze(2).to_broadcast([P, SEQ_TILES, STEPS]),
            op0=ALU.mult,
            op1=ALU.mult,
        )
        wide = [P, SEQ_TILES * PAIRS]
        turns = const.tile(wide, F32)
        whole_turns = const.tile(wide, F32)
        part_turns = const.tile(wide, F32)
        minus_size = const.tile(wide, F32)
        sin_table = const.tile([P, SEQ_TILES, PAIRS], F32)
        cos_table = const.tile([P, SEQ_TILES, PAIRS], F32)

        def table_step(i):
            if i == 0:
                nc.vector.tensor_tensor(
                    out=turns[:].rearrange("p (c b) -> p c b", b=STEPS),
                    in0=coarse_turns[:]
                    .rearrange("p t a -> p (t a)")
                    .unsqueeze(2)
                    .to_broadcast([P, SEQ_TILES * STEPS, STEPS]),
                    in1=powers[:, 1, :].unsqueeze(1).to_broadcast([P, SEQ_TILES * STEPS, STEPS]),
                    op=ALU.mult,
                )
            elif i == 1:
                nc.vector.tensor_scalar(
                    out=whole_turns[:],
                    in0=turns[:],
                    scalar1=ROUND_MAGIC,
                    scalar2=ROUND_MAGIC,
                    op0=ALU.add,
                    op1=ALU.subtract,
                )
            elif i == 2:
                nc.vector.tensor_tensor(
                    out=part_turns[:], in0=turns[:], in1=whole_turns[:], op=ALU.subtract
                )
            elif i == 3:
                nc.vector.scalar_tensor_tensor(
                    out=minus_size[:],
                    in0=part_turns[:],
                    scalar=-1.0,
                    in1=part_turns[:],
                    op0=ALU.mult,
                    op1=ALU.min,
                )

        def sines():
            nc.scalar.activation(
                out=sin_table[:].rearrange("p t j -> p (t j)"),
                in_=part_turns[:],
                func=ACT.Sin,
                scale=TWO_PI,
            )
            nc.scalar.activation(
                out=cos_table[:].rearrange("p t j -> p (t j)"),
                in_=minus_size[:],
                func=ACT.Sin,
                scale=TWO_PI,
                bias=half_pi[:, 0:1],
            )

        def sort_words(rows):
            ordered = stage.tile([P, BANKS_PER_TILE, 2, 2, P], F32)
            nc.vector.tensor_copy(
                out=ordered[:].rearrange("p h g u q -> p (h g) u q"),
                in_=rows[:].bitcast(F32).rearrange("p (c q u) -> p c u q", q=P, u=2),
            )
            return ordered

        def transpose_rows(blocks, layout, copies):
            grouped = stage.tile([P, PASSES * P * 4], BF16, align_bytes=64)
            grouped_words = grouped[:].bitcast(F32).rearrange(
                layout, h=BANKS_PER_TILE, g=2, u=2
            )
            for h in range(BANKS_PER_TILE):
                bank = psum_t.tile([P, 2, 2, P], F32, tag="bank")
                for g in range(2):
                    for u in range(2):
                        nc.tensor.transpose(bank[:, g, u, :], blocks(h, g, u), identity[:])
                copies[h](
                    out=grouped_words[:, h],
                    in_=bank[:].rearrange("p g u r -> p g r u"),
                )
            return grouped

        def as_sorted(ordered):
            return lambda h, g, u: ordered[:, h, g, u, :]

        def as_loaded(rows):
            words = rows[:].bitcast(F32).rearrange(
                "p (h g q u) -> p h g u q", h=BANKS_PER_TILE, g=2, u=2
            )
            return lambda h, g, u: words[:, h, g, u, :]

        w_codes = quant.tile([P, PASSES, LATENT + ROPE], U32, align_bytes=64)
        w_scales = quant.tile([P, PASSES, LATENT + ROPE], U8, align_bytes=64)

        def quantise_weights(n, grouped):
            if n < W_TILES - 1:
                rows, half = divmod(n, 2)
                passes, first, count = [2 * half, 2 * half + 1], rows * UNIT_ROWS, UNIT_ROWS
            else:
                passes, first, count = list(range(PASSES)), LATENT, ROPE
            for i, g in enumerate(passes):
                nc.vector.quantize_mx(
                    out=w_codes[:, g, first : first + count].bitcast(FP8X4),
                    scales=w_scales[:, g, first : first + count],
                    in_=grouped[:, i * 4 * count : (i + 1) * 4 * count],
                )

        x_codes = {}
        x_scales = {}

        def quantise_tokens(m, grouped):
            x_codes[m] = quant.tile([P, PASSES * P], U32, align_bytes=64, name="x_codes", bufs=X_TILES)
            x_scales[m] = quant.tile([P, PASSES * P], U8, align_bytes=64, name="x_scales", bufs=X_TILES)
            nc.vector.quantize_mx(
                out=x_codes[m][:].bitcast(FP8X4), scales=x_scales[m][:], in_=grouped[:]
            )

        def multiply(m, out, columns, passes=range(PASSES)):
            for g in passes:
                nc.tensor.matmul_mx(
                    out=out,
                    lhsT=x_codes[m][:, g * P : (g + 1) * P].bitcast(FP8X4),
                    lhsT_scale=x_scales[m][:, g * P : (g + 1) * P],
                    rhs=w_codes[:, g, columns].bitcast(FP8X4),
                    rhs_scale=w_scales[:, g, columns],
                    start=(g == 0),
                    stop=(g == PASSES - 1),
                )

        sum_squares = {}
        inverse_rms = {}

        def square(m):
            squares = work.tile([P, LATENT], BF16)
            sum_squares[m] = work.tile([P, 1], F32, name="sum_squares")
            nc.scalar.activation(
                out=squares[:], in_=latent[m][:], func=ACT.Square, accum_out=sum_squares[m][:]
            )
            inverse_rms[m] = work.tile([P, 1], F32, name="inverse_rms")
            nc.scalar.activation(
                out=inverse_rms[m][:],
                in_=sum_squares[m][:],
                func=ACT.Abs_reciprocal_sqrt,
                scale=1.0 / LATENT,
                bias=eps[:, 0:1],
            )

        def normalise(m):
            kv_cache = work.tile([P, LATENT], F32, bufs=4)
            nc.vector.scalar_tensor_tensor(
                out=kv_cache[:],
                in0=latent[m][:],
                scalar=inverse_rms[m][:, 0:1],
                in1=gain[:],
                op0=ALU.mult,
                op1=ALU.mult,
            )
            nc.sync.dma_start(out=kv_cache_rows[m * P : (m + 1) * P, :], in_=kv_cache[:])

        def rotation_products(t, count, raw_keys):
            pairs = raw_keys[:].rearrange("p t (j e) -> p (t j) e", e=2)
            sines = sin_table[:, t : t + count].rearrange("p t j -> p (t j)")
            cosines = cos_table[:, t : t + count].rearrange("p t j -> p (t j)")
            with_cos = work.tile([P, count * PAIRS, 2], F32, name="with_cos%d" % count)
            nc.vector.tensor_tensor(
                out=with_cos[:],
                in0=pairs,
                in1=cosines.unsqueeze(2).to_broadcast([P, count * PAIRS, 2]),
                op=ALU.mult,
            )
            with_sin = work.tile([P, 2, count * PAIRS], F32, name="with_sin%d" % count)
            nc.vector.scalar_tensor_tensor(
                out=with_sin[:, 0, :],
                in0=pairs[:, :, 1],
                scalar=-1.0,
                in1=sines,
                op0=ALU.mult,
                op1=ALU.mult,
            )
            nc.vector.tensor_tensor(
                out=with_sin[:, 1, :], in0=pairs[:, :, 0], in1=sines, op=ALU.mult
            )
            return with_cos, with_sin

        def rotation_sum(m, count, with_cos, with_sin):
            k_pe = work.tile([P, count * PAIRS, 2], F32, name="k_pe%d" % count)
            nc.vector.tensor_tensor(
                out=k_pe[:], in0=with_cos[:], in1=with_sin[:].rearrange("p e c -> p c e"), op=ALU.add
            )
            nc.sync.dma_start(
                out=k_pe_rows[m * P : (m + count) * P, :].rearrange("(t p) c -> p t c", p=P),
                in_=k_pe[:].rearrange("p (t j) e -> p t (j e)", t=count),
            )

        order = [("x", m) for m in range(FIRST_TILES)]
        order += [("w", n) for n in range(W_TILES)]
        order += [("x", m) for m in range(FIRST_TILES, X_TILES)]
        shared_copies = [nc.vector.tensor_copy, nc.scalar.copy]
        scalar_copies = [nc.scalar.copy, nc.scalar.copy]
        vector_copies = [nc.vector.tensor_copy, nc.vector.tensor_copy]
        grouped = {}

        sorted_words = {}

        def rows_of(i):
            kind, tile_index = order[i]
            return x_raw[tile_index] if kind == "x" else w_raw[tile_index]

        def sort_next(i):
            if i < len(order):
                sorted_words[i] = sort_words(rows_of(i))

        def transpose_next(i, copies):
            if i < len(order):
                blocks = as_sorted(sorted_words[i]) if i in sorted_words else as_loaded(rows_of(i))
                kind, tile_index = order[i]
                latent_weights = kind == "w" and tile_index < W_TILES - 1
                layout = "p (g h r u) -> p h g r u" if latent_weights else "p (h g r u) -> p h g r u"
                grouped[i] = transpose_rows(blocks, layout, copies)

        def quantise_next(i):
            if i < len(order):
                kind, tile_index = order[i]
                if kind == "x":
                    quantise_tokens(tile_index, grouped[i])
                else:
                    quantise_weights(tile_index, grouped[i])

        early_copies = [shared_copies, shared_copies, scalar_copies, scalar_copies, scalar_copies]
        for i in range(FIRST_TILES + LEAD):
            transpose_next(i, early_copies[i])
            if i > 0:
                quantise_next(i - 1)
            table_step(i)

        sines()
        nc.scalar.activation(out=table_warmer[:], in_=eps[:], func=ACT.Abs_reciprocal_sqrt)

        latent = {}
        raw_keys = {}
        rotation = {}
        for m in range(FIRST_TILES):
            latent[m] = psum_lat.tile([P, LATENT], F32, name="latent")
        together = {0: 4, 4: 2, 6: 1, 7: 1}
        first_of = {m: start for start in together for m in range(start, start + together[start])}

        def keys_of(m):
            start = first_of[m]
            if start not in raw_keys:
                pool = psum_t if start >= 6 else psum_rope
                raw_keys[start] = pool.tile(
                    [P, together[start], ROPE],
                    F32,
                    name="raw_keys%d" % start,
                    tag="bank" if start >= 6 else "raw_keys",
                )
            return raw_keys[start][:, m - start, :]

        def multiply_weights(n):
            for m in range(FIRST_TILES):
                if n < W_TILES - 1:
                    rows, half = divmod(n, 2)
                    columns = slice(rows * UNIT_ROWS, (rows + 1) * UNIT_ROWS)
                    multiply(m, latent[m][:, columns], columns, [2 * half, 2 * half + 1])
                else:
                    multiply(m, keys_of(m), slice(LATENT, LATENT + ROPE))

        def multiply_tokens(m):
            if m in (5, 6):
                latent[m] = psum_t.tile([P, LATENT], F32, name="late_latent", tag="bank")
            else:
                latent[m] = psum_lat.tile([P, LATENT], F32, name="latent")
            multiply(m, latent[m][:], slice(0, LATENT))
            multiply(m, keys_of(m), slice(LATENT, LATENT + ROPE))

        HALF = LATENT // 2
        last = X_TILES - 1
        half_banks = []

        def multiply_last():
            for half in range(2):
                bank = psum_lat.tile([P, LATENT], F32, name="half_bank", tag="latent")
                half_banks.append(bank)
                columns = slice(half * HALF, (half + 1) * HALF)
                multiply(last, bank[:, 0:HALF], columns)
            multiply(last, keys_of(last), slice(LATENT, LATENT + ROPE))

        def square_last():
            for half in range(2):
                squares = work.tile([P, LATENT], BF16)
                half_sum = work.tile([P, 1], F32)
                nc.scalar.activation(
                    out=squares[:, 0:HALF],
                    in_=half_banks[half][:, 0:HALF],
                    func=ACT.Square,
                    accum_out=half_sum[:],
                )
                if half == 0:
                    share = work.tile([P, 1], F32)
                    nc.gpsimd.tensor_scalar(
                        out=share[:],
                        in0=half_sum[:],
                        scalar1=1.0 / LATENT,
                        scalar2=EPS,
                        op0=ALU.mult,
                        op1=ALU.add,
                    )
            inverse_rms[last] = work.tile([P, 1], F32, name="inverse_rms")
            nc.scalar.activation(
                out=inverse_rms[last][:],
                in_=half_sum[:],
                func=ACT.Abs_reciprocal_sqrt,
                scale=1.0 / LATENT,
                bias=share[:, 0:1],
            )

        def normalise_last():
            queues = [nc.sync, nc.scalar]
            for half in range(2):
                columns = slice(half * HALF, (half + 1) * HALF)
                kv_half = work.tile([P, HALF], F32, bufs=2)
                nc.vector.scalar_tensor_tensor(
                    out=kv_half[:],
                    in0=half_banks[half][:, 0:HALF],
                    scalar=inverse_rms[last][:, 0:1],
                    in1=gain[:, columns],
                    op0=ALU.mult,
                    op1=ALU.mult,
                )
                queues[half].dma_start(
                    out=kv_cache_rows[last * P : (last + 1) * P, columns], in_=kv_half[:]
                )

        def rotate(start):
            rotation[start] = rotation_products(
                start % SEQ_TILES, together[start], raw_keys[start]
            )

        def finish_rotation(start):
            rotation_sum(start, together[start], *rotation[start])

        multiply_weights(0)
        quantise_next(4)
        transpose_next(5, shared_copies)
        sort_next(7)
        multiply_weights(1)
        quantise_next(5)
        transpose_next(6, scalar_copies)
        sort_next(8)
        multiply_weights(2)
        transpose_next(7, scalar_copies)
        quantise_next(6)
        sort_next(9)
        multiply_weights(3)
        transpose_next(8, scalar_copies)
        sort_next(10)
        quantise_next(7)
        square(0)
        square(1)
        multiply_weights(4)
        transpose_next(9, scalar_copies)
        quantise_next(8)
        transpose_next(10, scalar_copies)
        normalise(0)
        sort_next(11)
        normalise(1)
        multiply_tokens(2)
        multiply_tokens(3)
        quantise_next(9)
        square(2)
        transpose_next(11, scalar_copies)
        square(3)
        rotate(0)
        quantise_next(10)
        transpose_next(12, scalar_copies)
        normalise(2)
        quantise_next(11)
        multiply_tokens(4)
        square(4)
        normalise(3)
        quantise_next(12)
        finish_rotation(0)
        multiply_tokens(5)
        square(5)
        normalise(4)
        rotate(4)
        multiply_tokens(6)
        square(6)
        normalise(5)
        finish_rotation(4)
        multiply_last()
        square_last()
        rotate(6)
        normalise(6)
        rotate(7)
        normalise_last()
        finish_rotation(6)
        finish_rotation(7)
